import numpy as np
import ml_dtypes


def mxq(x, axis, fmt="e4m3"):
    dtype, down = {"e4m3": (ml_dtypes.float8_e4m3fn, 7), "e5m2": (ml_dtypes.float8_e5m2, 14)}[fmt]
    v = np.moveaxis(np.asarray(x, np.float32).astype(ml_dtypes.bfloat16).astype(np.float64), axis, -1)
    blocks = v.reshape(v.shape[:-1] + (-1, 32))
    amax = np.abs(blocks).max(-1, keepdims=True)
    byte = np.maximum(np.where(amax > 0, np.frexp(amax)[1] - 1 + 127, 0) - down, 1)
    scale = np.exp2(byte - 127.0)
    codes = (blocks / scale).astype(np.float32).astype(dtype).astype(np.float64)
    return np.moveaxis((codes * scale).reshape(v.shape), -1, axis)


WIDE = False


def mx_kscale(k):
    if not WIDE:
        return np.ones(k)
    levels = np.array([10, -10, 5, -5, 0])
    a = np.random.permutation(np.resize(levels, k // 512 * 4)).reshape(k // 512, 4)
    idx = np.arange(k)
    return np.exp2(a[idx // 512, idx % 128 // 32])


BF16 = ml_dtypes.bfloat16


def bf(x):
    return np.asarray(x, np.float32).astype(BF16)


def f64(x):
    return np.asarray(x).astype(np.float64)


B, C, H, W, O = 2, 256, 128, 128, 512
K = 4 * C


def haar_dwt2(x):
    nb, nc_, nh, nw = x.shape
    xr = x.reshape(nb, nc_, nh // 2, 2, nw // 2, 2)
    a = xr[:, :, :, 0, :, 0]
    b = xr[:, :, :, 0, :, 1]
    c = xr[:, :, :, 1, :, 0]
    d = xr[:, :, :, 1, :, 1]
    half = 0.5
    LL = (a + b + c + d) * half
    LH = (a + b - c - d) * half
    HL = (a - b + c - d) * half
    HH = (a - b - c + d) * half
    return LL, LH, HL, HH


def setup_inputs():
    sc = mx_kscale(K)[::4]
    sk = np.repeat(sc, 4)
    return {"x": bf(np.random.standard_normal((B, C, H, W)) * sc[None, :, None, None]),
            "w_fusion": bf(np.random.standard_normal((O, K, 1, 1)) / np.sqrt(K) / sk[None, :, None, None])}


def reference(x, w_fusion):
    x = f64(x)
    nb, nc_, nh, nw = x.shape
    LL, LH, HL, HH = haar_dwt2(x)
    combined = np.stack([LL, LH, HL, HH], axis=2)
    combined = combined.reshape(nb, nc_ * 4, nh // 2, nw // 2)
    w = f64(w_fusion)[:, :, 0, 0]
    return np.einsum('bchw,oc->bohw', mxq(combined, 1, "e4m3"), mxq(w, 1, "e4m3"), optimize=True)

@@ -1,0 +1,160 @@
+from contextlib import ExitStack
+
+import concourse.mybir as mybir
+from concourse.masks import make_identity
+
+FLOPS = 2 * 2 * 4096 * 1024 * 512
+
+F32 = mybir.dt.float32
+BF16 = mybir.dt.bfloat16
+U32 = mybir.dt.uint32
+U8 = mybir.dt.uint8
+FP8X4 = mybir.dt.float8_e4m3fn_x4
+ADD = mybir.AluOpType.add
+SUB = mybir.AluOpType.subtract
+COPY = mybir.ActivationFunctionType.Copy
+
+P = 128
+G = 2
+MT = 4
+NPIX = 512
+UNITS_PER_IMAGE = 8
+UNITS = 2 * UNITS_PER_IMAGE
+
+
+def tile_haarwaveletlayer_t_kernel(tc, x, w_fusion, out):
+    nc = tc.nc
+    with ExitStack() as ctx:
+        const = ctx.enter_context(tc.tile_pool(name="const", bufs=1))
+        xpool = ctx.enter_context(tc.tile_pool(name="xpool", bufs=4))
+        tpool = ctx.enter_context(tc.tile_pool(name="tpool", bufs=2))
+        plpool = ctx.enter_context(tc.tile_pool(name="plpool", bufs=2))
+        grpool = ctx.enter_context(tc.tile_pool(name="grpool", bufs=2))
+        qpool = ctx.enter_context(tc.tile_pool(name="qpool", bufs=2))
+        opool = ctx.enter_context(tc.tile_pool(name="opool", bufs=3))
+        accpool = ctx.enter_context(tc.psum_pool(name="accpool", bufs=6))
+        auxpool = ctx.enter_context(tc.psum_pool(name="auxpool", bufs=2))
+
+        x_tiles = {}
+        t_tiles = {}
+        pl_tiles = {}
+        gr_tiles = {}
+        q_tiles = {}
+
+        def load(u):
+            n, r = divmod(u, UNITS_PER_IMAGE)
+            xt = xpool.tile([P, G * 2048], BF16, name="xt")
+            src = x[n].rearrange("(g p) h w -> p g (h w)", g=G)
+            nc.sync.dma_start(
+                out=xt[:].rearrange("p (g f) -> p g f", g=G),
+                in_=src[:, :, 2048 * r : 2048 * (r + 1)],
+            )
+            x_tiles[u] = xt
+
+        def stage1(u):
+            xv = x_tiles[u][:].rearrange("p (a d w) -> p a d w", d=2, w=128)
+            tt = tpool.tile([P, 2, 2048], F32, name="tt")
+            for v, op in ((0, ADD), (1, SUB)):
+                nc.vector.tensor_tensor(
+                    out=tt[:, v, :].rearrange("p (a w) -> p a w", w=128),
+                    in0=xv[:, :, 0, :],
+                    in1=xv[:, :, 1, :],
+                    op=op,
+                )
+            t_tiles[u] = tt
+
+        def stage2(u):
+            tv = t_tiles[u][:].rearrange("p v (r e) -> p (v r) e", e=2)
+            pl = plpool.tile([P, 4 * G * NPIX], BF16, name="pl")
+            for h, op in ((0, ADD), (1, SUB)):
+                nc.vector.tensor_tensor(
+                    out=pl[:, 2048 * h : 2048 * (h + 1)],
+                    in0=tv[:, :, 0],
+                    in1=tv[:, :, 1],
+                    op=op,
+                )
+            pl_tiles[u] = pl
+
+        def regroup(u):
+            gr = grpool.tile([P, 4 * G * NPIX], BF16, name="gr", align_bytes=64)
+            nc.scalar.activation(
+                out=gr[:].rearrange("p (r t) -> p r t", t=4),
+                in_=pl_tiles[u][:].rearrange("p (t r) -> p r t", t=4),
+                func=COPY,
+                scale=0.5,
+            )
+            gr_tiles[u] = gr
+
+        def quantise(u):
+            codes = qpool.tile([P, G * NPIX], U32, name="codes", align_bytes=64)
+            scales = qpool.tile([P, G * NPIX], U8, name="scales", align_bytes=64)
+            nc.vector.quantize_mx(out=codes[:].bitcast(FP8X4), scales=scales[:], in_=gr_tiles[u][:])
+            q_tiles[u] = (codes, scales)
+
+        def multiply(u):
+            n, r = divmod(u, UNITS_PER_IMAGE)
+            codes, scales = q_tiles[u]
+            ot = opool.tile([P, MT, NPIX], F32, name="ot")
+            for m in range(MT):
+                acc = accpool.tile([P, NPIX], F32, name="acc")
+                for g in range(G):
+                    wcols = slice(512 * g + P * m, 512 * g + P * (m + 1))
+                    xcols = slice(NPIX * g, NPIX * (g + 1))
+                    nc.tensor.matmul_mx(
+                        out=acc[:],
+                        lhsT=w_codes[:, wcols].bitcast(FP8X4),
+                        lhsT_scale=w_scales[:, wcols],
+                        rhs=codes[:, xcols].bitcast(FP8X4),
+                        rhs_scale=scales[:, xcols],
+                        start=(g == 0),
+                        stop=(g == G - 1),
+                    )
+                nc.scalar.copy(out=ot[:, m, :], in_=acc[:])
+            dst = out[n].rearrange("(m p) i j -> p m (i j)", m=MT)
+            nc.scalar.dma_start(out=dst[:, :, NPIX * r : NPIX * (r + 1)], in_=ot[:])
+
+        load(0)
+        w_sb = const.tile([P, MT * 1024], BF16, name="w_sb")
+        nc.sync.dma_start(
+            out=w_sb[:].rearrange("p (m k) -> p m k", m=MT),
+            in_=w_fusion.rearrange("(m p) k a b -> p m (k a b)", m=MT),
+        )
+        load(1)
+        load(2)
+
+        ident = const.tile([P, P], F32, name="ident")
+        make_identity(nc, ident[:])
+
+        w32 = w_sb[:].bitcast(F32)
+        w_grouped = const.tile([P, G * 512 * 4], BF16, name="w_grouped", align_bytes=64)
+        wg32 = w_grouped[:].bitcast(F32)
+        for g in range(G):
+            for mp in range(MT // 2):
+                wt = auxpool.tile([P, 2, 2, P], F32, name="wt")
+                for mm in range(2):
+                    for uu in range(2):
+                        first = 512 * (2 * mp + mm) + 256 * g + uu
+                        nc.tensor.transpose(wt[:, mm, uu, :], w32[:, first : first + 255 : 2], ident[:])
+                nc.scalar.copy(
+                    out=wg32[:, 1024 * g + 512 * mp : 1024 * g + 512 * (mp + 1)].rearrange(
+                        "p (m o u) -> p m o u", m=2, u=2
+                    ),
+                    in_=wt[:].rearrange("p m u o -> p m o u"),
+                )
+        w_codes = const.tile([P, G * 512], U32, name="w_codes", align_bytes=64)
+        w_scales = const.tile([P, G * 512], U8, name="w_scales", align_bytes=64)
+
+        stage1(0)
+        for u in range(UNITS + 1):
+            if u + 3 < UNITS:
+                load(u + 3)
+            if u + 1 < UNITS:
+                stage1(u + 1)
+            if u < UNITS:
+                stage2(u)
+                regroup(u)
+            if u == 0:
+                nc.vector.quantize_mx(out=w_codes[:].bitcast(FP8X4), scales=w_scales[:], in_=w_grouped[:])
+            if u >= 1:
+                quantise(u - 1)
+                multiply(u - 1)

@@ -17,9 +17,23 @@ COPY = mybir.ActivationFunctionType.Copy
 P = 128
 G = 2
 MT = 4
-NPIX = 512
-UNITS_PER_IMAGE = 8
-UNITS = 2 * UNITS_PER_IMAGE
+BANK = 512
+
+A_CHUNKS = (
+    [(0, 0, 128), (0, 128, 128), (0, 256, 256)]
+    + [(0, 512 * r, 512) for r in range(1, 8)]
+    + [(1, 512 * r, 512) for r in range(4)]
+    + [(1, 2048, 256), (1, 2304, 128), (1, 2432, 128)]
+)
+NA = len(A_CHUNKS)
+REGROUP_ON_VECTOR = (NA - 3, NA - 2, NA - 1)
+B_IMAGE = 1
+B_FIRST_ROW = 40
+B_ROWS = 24
+B_UNITS = 3
+B_ITEM_STEPS = range(4, 12)
+B_ITEMS_PER_STEP = 3
+B_QUANTISE_STEP = (7, 10, 12)
 
 
 def tile_haarwaveletlayer_t_kernel(tc, x, w_fusion, out):
@@ -30,30 +44,34 @@ def tile_haarwaveletlayer_t_kernel(tc, x, w_fusion, out):
         tpool = ctx.enter_context(tc.tile_pool(name="tpool", bufs=2))
         plpool = ctx.enter_context(tc.tile_pool(name="plpool", bufs=2))
         grpool = ctx.enter_context(tc.tile_pool(name="grpool", bufs=2))
-        qpool = ctx.enter_context(tc.tile_pool(name="qpool", bufs=2))
+        grbpool = ctx.enter_context(tc.tile_pool(name="grbpool", bufs=2))
+        qpool = ctx.enter_context(tc.tile_pool(name="qpool", bufs=4))
         opool = ctx.enter_context(tc.tile_pool(name="opool", bufs=3))
         accpool = ctx.enter_context(tc.psum_pool(name="accpool", bufs=6))
         auxpool = ctx.enter_context(tc.psum_pool(name="auxpool", bufs=2))
+        ctx.enter_context(tc.manual_schedule())
 
         x_tiles = {}
         t_tiles = {}
         pl_tiles = {}
         gr_tiles = {}
         q_tiles = {}
+        acc_tiles = {}
 
-        def load(u):
-            n, r = divmod(u, UNITS_PER_IMAGE)
-            xt = xpool.tile([P, G * 2048], BF16, name="xt")
+        def load(i):
+            n, p0, npx = A_CHUNKS[i]
+            xt = xpool.tile([P, G * 4 * npx], BF16, name="xt")
             src = x[n].rearrange("(g p) h w -> p g (h w)", g=G)
             nc.sync.dma_start(
                 out=xt[:].rearrange("p (g f) -> p g f", g=G),
-                in_=src[:, :, 2048 * r : 2048 * (r + 1)],
+                in_=src[:, :, 4 * p0 : 4 * (p0 + npx)],
             )
-            x_tiles[u] = xt
+            x_tiles[i] = xt
 
-        def stage1(u):
-            xv = x_tiles[u][:].rearrange("p (a d w) -> p a d w", d=2, w=128)
-            tt = tpool.tile([P, 2, 2048], F32, name="tt")
+        def vertical(i):
+            npx = A_CHUNKS[i][2]
+            xv = x_tiles[i][:].rearrange("p (a d w) -> p a d w", d=2, w=128)
+            tt = tpool.tile([P, 2, G * 2 * npx], F32, name="tt")
             for v, op in ((0, ADD), (1, SUB)):
                 nc.vector.tensor_tensor(
                     out=tt[:, v, :].rearrange("p (a w) -> p a w", w=128),
@@ -61,100 +79,239 @@ def tile_haarwaveletlayer_t_kernel(tc, x, w_fusion, out):
                     in1=xv[:, :, 1, :],
                     op=op,
                 )
-            t_tiles[u] = tt
+            t_tiles[i] = tt
 
-        def stage2(u):
-            tv = t_tiles[u][:].rearrange("p v (r e) -> p (v r) e", e=2)
-            pl = plpool.tile([P, 4 * G * NPIX], BF16, name="pl")
+        def horizontal(i):
+            npx = A_CHUNKS[i][2]
+            half = 2 * G * npx
+            tv = t_tiles[i][:].rearrange("p v (r e) -> p (v r) e", e=2)
+            pl = plpool.tile([P, 2 * half], BF16, name="pl")
             for h, op in ((0, ADD), (1, SUB)):
                 nc.vector.tensor_tensor(
-                    out=pl[:, 2048 * h : 2048 * (h + 1)],
+                    out=pl[:, half * h : half * (h + 1)],
                     in0=tv[:, :, 0],
                     in1=tv[:, :, 1],
                     op=op,
                 )
-            pl_tiles[u] = pl
+            pl_tiles[i] = pl
 
-        def regroup(u):
-            gr = grpool.tile([P, 4 * G * NPIX], BF16, name="gr", align_bytes=64)
+        def regroup(i):
+            npx = A_CHUNKS[i][2]
+            gr = grpool.tile([P, 4 * G * npx], BF16, name="gr", align_bytes=64)
+            dst = gr[:].rearrange("p (c i t) -> p c t i", i=4, t=4)
+            src = pl_tiles[i][:].rearrange("p (t c i) -> p c t i", t=4, i=4)
+            if i in REGROUP_ON_VECTOR:
+                nc.vector.tensor_scalar_mul(out=dst, in0=src, scalar1=0.5)
+            else:
+                nc.scalar.activation(out=dst, in_=src, func=COPY, scale=0.5)
+            gr_tiles[("a", i)] = gr
+
+        xb = const.tile([P, 4, B_ROWS * 128], BF16, name="xb")
+
+        def load_b(cg):
+            rows = x[B_IMAGE].rearrange("c (i d) w -> c d i w", d=2)
+            for di in range(2):
+                nc.sync.dma_start(
+                    out=xb[di:P:2, cg, :].rearrange("p (i w) -> p i w", w=128),
+                    in_=rows[64 * cg : 64 * (cg + 1), di, B_FIRST_ROW : B_FIRST_ROW + B_ROWS, :],
+                )
+
+        def haar_item(item):
+            k, rest = divmod(item, 8)
+            g, q = divmod(rest, 4)
+            if rest == 0:
+                gr_tiles[("b", k)] = grbpool.tile([P, 4 * G * 512], BF16, name="grb", align_bytes=64)
+            hb = auxpool.tile([P, 4, P], F32, name="hb", tag="aux")
+            first = (8 * k + 2 * q) * 128
+            for e in range(2):
+                pair = xb[:, 2 * g + e, first : first + 256].rearrange("p (r c) -> p r c", c=2)
+                for sh in range(2):
+                    t = 2 * e + sh
+                    nc.tensor.matmul(hb[:, t, :], lhsT=sv[:], rhs=pair[:, :, 0], start=True, stop=False)
+                    nc.tensor.matmul(
+                        hb[:, t, :], lhsT=(sv[:] if sh == 0 else svn[:]), rhs=pair[:, :, 1], start=False, stop=True
+                    )
+            c0 = 4 * (512 * g + 128 * q)
             nc.scalar.activation(
-                out=gr[:].rearrange("p (r t) -> p r t", t=4),
-                in_=pl_tiles[u][:].rearrange("p (t r) -> p r t", t=4),
+                out=gr_tiles[("b", k)][:, c0 : c0 + 512].rearrange("p (r t) -> p r t", t=4),
+                in_=hb[:].rearrange("p t r -> p r t"),
                 func=COPY,
                 scale=0.5,
             )
-            gr_tiles[u] = gr
 
-        def quantise(u):
-            codes = qpool.tile([P, G * NPIX], U32, name="codes", align_bytes=64)
-            scales = qpool.tile([P, G * NPIX], U8, name="scales", align_bytes=64)
-            nc.vector.quantize_mx(out=codes[:].bitcast(FP8X4), scales=scales[:], in_=gr_tiles[u][:])
-            q_tiles[u] = (codes, scales)
+        def place(job):
+            if job[0] == "a":
+                return A_CHUNKS[job[1]]
+            return (B_IMAGE, 64 * B_FIRST_ROW + 512 * job[1], 512)
 
-        def multiply(u):
-            n, r = divmod(u, UNITS_PER_IMAGE)
-            codes, scales = q_tiles[u]
-            ot = opool.tile([P, MT, NPIX], F32, name="ot")
-            for m in range(MT):
-                acc = accpool.tile([P, NPIX], F32, name="acc")
-                for g in range(G):
-                    wcols = slice(512 * g + P * m, 512 * g + P * (m + 1))
-                    xcols = slice(NPIX * g, NPIX * (g + 1))
-                    nc.tensor.matmul_mx(
-                        out=acc[:],
-                        lhsT=w_codes[:, wcols].bitcast(FP8X4),
-                        lhsT_scale=w_scales[:, wcols],
-                        rhs=codes[:, xcols].bitcast(FP8X4),
-                        rhs_scale=scales[:, xcols],
-                        start=(g == 0),
-                        stop=(g == G - 1),
-                    )
-                nc.scalar.copy(out=ot[:, m, :], in_=acc[:])
+        def quantise(job):
+            npx = place(job)[2]
+            codes = qpool.tile([P, G * npx], U32, name="codes", align_bytes=64)
+            scales = qpool.tile([P, G * npx], U8, name="scales", align_bytes=64)
+            nc.vector.quantize_mx(out=codes[:].bitcast(FP8X4), scales=scales[:], in_=gr_tiles[job][:])
+            q_tiles[job] = (codes, scales)
+
+        def multiply(job):
+            npx = place(job)[2]
+            codes, scales = q_tiles[job]
+            wc, ws = w_quantised[job[0]]
+            per_bank = BANK // npx
+            banks = []
+            for b in range(MT // per_bank):
+                acc = accpool.tile([P, per_bank, npx], F32, name="acc", tag="acc")
+                for s in range(per_bank):
+                    m = b * per_bank + s
+                    for g in range(G):
+                        wcols = slice(512 * g + P * m, 512 * g + P * (m + 1))
+                        xcols = slice(npx * g, npx * (g + 1))
+                        nc.tensor.matmul_mx(
+                            out=acc[:, s, :],
+                            lhsT=wc[:, wcols].bitcast(FP8X4),
+                            lhsT_scale=ws[:, wcols],
+                            rhs=codes[:, xcols].bitcast(FP8X4),
+                            rhs_scale=scales[:, xcols],
+                            start=(g == 0),
+                            stop=(g == G - 1),
+                        )
+                banks.append(acc)
+            acc_tiles[job] = banks
+
+        def evacuate(job):
+            n, p0, npx = place(job)
+            per_bank = BANK // npx
+            ot = opool.tile([P, MT, npx], F32, name="ot")
+            for b, acc in enumerate(acc_tiles[job]):
+                nc.scalar.copy(out=ot[:, b * per_bank : (b + 1) * per_bank, :], in_=acc[:])
             dst = out[n].rearrange("(m p) i j -> p m (i j)", m=MT)
-            nc.scalar.dma_start(out=dst[:, :, NPIX * r : NPIX * (r + 1)], in_=ot[:])
+            nc.scalar.dma_start(out=dst[:, :, p0 : p0 + npx], in_=ot[:])
+
+        w_sb = const.tile([P, MT * 1024], BF16, name="w_sb")
+        w_sorted = const.tile([P, MT * 1024], BF16, name="w_sorted")
+        w_grouped = {
+            "a": const.tile([P, G * 512 * 4], BF16, name="w_grouped_a", align_bytes=64),
+            "b": const.tile([P, G * 512 * 4], BF16, name="w_grouped_b", align_bytes=64),
+        }
+        w_quantised = {
+            "a": (
+                const.tile([P, G * 512], U32, name="w_codes_a", align_bytes=64),
+                const.tile([P, G * 512], U8, name="w_scales_a", align_bytes=64),
+            ),
+            "b": (
+                const.tile([P, G * 512], U32, name="w_codes_b", align_bytes=64),
+                const.tile([P, G * 512], U8, name="w_scales_b", align_bytes=64),
+            ),
+        }
+
+        def sort_w():
+            nc.scalar.copy(
+                out=w_sorted[:].bitcast(F32).rearrange("p (a s q) -> p a s q", s=2, q=128),
+                in_=w_sb[:].bitcast(F32).rearrange("p (a q s) -> p a s q", s=2, q=128),
+            )
+
+        def transpose_w_a():
+            ws32 = w_sorted[:].bitcast(F32)
+            wg32 = w_grouped["a"][:].bitcast(F32)
+            for g in range(G):
+                for mp in range(MT // 2):
+                    wt = auxpool.tile([P, 2, 2, P], F32, name="wt", tag="aux")
+                    for mm in range(2):
+                        for s in range(2):
+                            first = ((2 * (2 * mp + mm) + g) * 2 + s) * 128
+                            nc.tensor.transpose(wt[:, mm, s, :], ws32[:, first : first + 128], ident32[:])
+                    nc.scalar.copy(
+                        out=wg32[:, 1024 * g + 512 * mp : 1024 * g + 512 * (mp + 1)].rearrange(
+                            "p (m o u) -> p m o u", m=2, u=2
+                        ),
+                        in_=wt[:].rearrange("p m u o -> p m o u"),
+                    )
+
+        def transpose_w_b():
+            for g in range(G):
+                for oh in range(2):
+                    wtb = auxpool.tile([P, 4, 256], BF16, name="wtb", tag="aux")
+                    for e in range(2):
+                        for sh in range(2):
+                            for mm in range(2):
+                                first = (((2 * (2 * oh + mm) + g) * 2 + sh) * 128 + 64 * e) * 2
+                                nc.tensor.transpose(
+                                    wtb[:, 2 * e + sh, P * mm : P * (mm + 1)],
+                                    w_sorted[:, first : first + 128],
+                                    identb[:],
+                                )
+                    nc.scalar.copy(
+                        out=w_grouped["b"][:, 2048 * g + 1024 * oh : 2048 * g + 1024 * (oh + 1)].rearrange(
+                            "p (o t) -> p o t", t=4
+                        ),
+                        in_=wtb[:].rearrange("p t o -> p o t"),
+                    )
+
+        def quantise_w(kind):
+            wc, ws = w_quantised[kind]
+            nc.vector.quantize_mx(out=wc[:].bitcast(FP8X4), scales=ws[:], in_=w_grouped[kind][:])
 
         load(0)
-        w_sb = const.tile([P, MT * 1024], BF16, name="w_sb")
+        load(1)
+        load(2)
         nc.sync.dma_start(
             out=w_sb[:].rearrange("p (m k) -> p m k", m=MT),
             in_=w_fusion.rearrange("(m p) k a b -> p m (k a b)", m=MT),
         )
-        load(1)
-        load(2)
+        load(3)
 
-        ident = const.tile([P, P], F32, name="ident")
-        make_identity(nc, ident[:])
+        ident32 = const.tile([P, P], F32, name="ident32")
+        make_identity(nc, ident32[:])
+        identb = const.tile([P, P], BF16, name="identb")
+        make_identity(nc, identb[:])
+        sv = const.tile([P, P], BF16, name="sv")
+        svn = const.tile([P, P], BF16, name="svn")
+        idv = identb[:].rearrange("p (c s) -> p c s", s=2)
+        svv = sv[:].rearrange("p (c s) -> p c s", s=2)
+        nc.vector.tensor_tensor(out=svv[:, :, 0], in0=idv[:, :, 0], in1=idv[:, :, 1], op=ADD)
+        nc.vector.tensor_tensor(out=svv[:, :, 1], in0=idv[:, :, 0], in1=idv[:, :, 1], op=SUB)
+        nc.vector.tensor_scalar_mul(out=svn[:], in0=sv[:], scalar1=-1.0)
 
-        w32 = w_sb[:].bitcast(F32)
-        w_grouped = const.tile([P, G * 512 * 4], BF16, name="w_grouped", align_bytes=64)
-        wg32 = w_grouped[:].bitcast(F32)
-        for g in range(G):
-            for mp in range(MT // 2):
-                wt = auxpool.tile([P, 2, 2, P], F32, name="wt")
-                for mm in range(2):
-                    for uu in range(2):
-                        first = 512 * (2 * mp + mm) + 256 * g + uu
-                        nc.tensor.transpose(wt[:, mm, uu, :], w32[:, first : first + 255 : 2], ident[:])
-                nc.scalar.copy(
-                    out=wg32[:, 1024 * g + 512 * mp : 1024 * g + 512 * (mp + 1)].rearrange(
-                        "p (m o u) -> p m o u", m=2, u=2
-                    ),
-                    in_=wt[:].rearrange("p m u o -> p m o u"),
-                )
-        w_codes = const.tile([P, G * 512], U32, name="w_codes", align_bytes=64)
-        w_scales = const.tile([P, G * 512], U8, name="w_scales", align_bytes=64)
+        vertical(0)
+        load(4)
+        load_b(0)
+        load_b(1)
 
-        stage1(0)
-        for u in range(UNITS + 1):
-            if u + 3 < UNITS:
-                load(u + 3)
-            if u + 1 < UNITS:
-                stage1(u + 1)
-            if u < UNITS:
-                stage2(u)
-                regroup(u)
-            if u == 0:
-                nc.vector.quantize_mx(out=w_codes[:].bitcast(FP8X4), scales=w_scales[:], in_=w_grouped[:])
-            if u >= 1:
-                quantise(u - 1)
-                multiply(u - 1)
+        due = [[] for step in range(NA + 4)]
+        item = 0
+        for i in range(NA + 3):
+            if i + 1 < NA:
+                vertical(i + 1)
+                if i + 5 < NA:
+                    load(i + 5)
+                if i == 0:
+                    load_b(2)
+                    load_b(3)
+            if i - 1 in REGROUP_ON_VECTOR:
+                regroup(i - 1)
+            if i < NA:
+                horizontal(i)
+            if 1 <= i <= NA and i - 1 not in REGROUP_ON_VECTOR:
+                regroup(i - 1)
+            if i == 1:
+                sort_w()
+            if i == 2:
+                transpose_w_a()
+            for job in due[i]:
+                multiply(job)
+                evacuate(job)
+            if i == 3:
+                transpose_w_b()
+            if i in B_ITEM_STEPS:
+                for rep in range(B_ITEMS_PER_STEP):
+                    haar_item(item)
+                    item += 1
+            if 1 <= i <= NA:
+                quantise(("a", i - 1))
+                due[max(i + 1, 3)].append(("a", i - 1))
+            if i == 2:
+                quantise_w("a")
+            if i == 4:
+                quantise_w("b")
+            if i in B_QUANTISE_STEP:
+                k = B_QUANTISE_STEP.index(i)
+                quantise(("b", k))
+                due[i + 1].append(("b", k))

@@ -19,32 +19,34 @@ G = 2
 MT = 4
 BANK = 512
 
+N_C = 6
+C_IMAGE = 1
+C_FIRST_ROW = 64 - 8 * N_C
+C_ITEMS = (0, 0, 4, 5, 5, 5, 5, 5, 5, 5, 5, 4)
+C_RUN = 895
+LAST_A = 512 * (7 - N_C)
 A_CHUNKS = (
     [(0, 0, 128), (0, 128, 128), (0, 256, 256)]
     + [(0, 512 * r, 512) for r in range(1, 8)]
-    + [(1, 512 * r, 512) for r in range(4)]
-    + [(1, 2048, 256), (1, 2304, 128), (1, 2432, 128)]
+    + [(1, 512 * r, 512) for r in range(7 - N_C)]
+    + [(1, LAST_A, 256), (1, LAST_A + 256, 128), (1, LAST_A + 384, 128)]
 )
 NA = len(A_CHUNKS)
-REGROUP_ON_VECTOR = (NA - 3, NA - 2, NA - 1)
-B_IMAGE = 1
-B_FIRST_ROW = 40
-B_ROWS = 24
-B_UNITS = 3
-B_ITEM_STEPS = range(4, 12)
-B_ITEMS_PER_STEP = 3
-B_QUANTISE_STEP = (7, 10, 12)
+assert sum(C_ITEMS) == 8 * N_C
+REGROUP_ON_VECTOR = tuple(range(NA - 5, NA))
 
 
 def tile_haarwaveletlayer_t_kernel(tc, x, w_fusion, out):
     nc = tc.nc
     with ExitStack() as ctx:
         const = ctx.enter_context(tc.tile_pool(name="const", bufs=1))
+        wgpool = ctx.enter_context(tc.tile_pool(name="wgpool", bufs=1))
         xpool = ctx.enter_context(tc.tile_pool(name="xpool", bufs=4))
+        xcpool = ctx.enter_context(tc.tile_pool(name="xcpool", bufs=3))
         tpool = ctx.enter_context(tc.tile_pool(name="tpool", bufs=2))
         plpool = ctx.enter_context(tc.tile_pool(name="plpool", bufs=2))
         grpool = ctx.enter_context(tc.tile_pool(name="grpool", bufs=2))
-        grbpool = ctx.enter_context(tc.tile_pool(name="grbpool", bufs=2))
+        grcpool = ctx.enter_context(tc.tile_pool(name="grcpool", bufs=2))
         qpool = ctx.enter_context(tc.tile_pool(name="qpool", bufs=4))
         opool = ctx.enter_context(tc.tile_pool(name="opool", bufs=3))
         accpool = ctx.enter_context(tc.psum_pool(name="accpool", bufs=6))
@@ -52,6 +54,7 @@ def tile_haarwaveletlayer_t_kernel(tc, x, w_fusion, out):
         ctx.enter_context(tc.manual_schedule())
 
         x_tiles = {}
+        xc_tiles = {}
         t_tiles = {}
         pl_tiles = {}
         gr_tiles = {}
@@ -106,43 +109,44 @@ def tile_haarwaveletlayer_t_kernel(tc, x, w_fusion, out):
                 nc.scalar.activation(out=dst, in_=src, func=COPY, scale=0.5)
             gr_tiles[("a", i)] = gr
 
-        xb = const.tile([P, 4, B_ROWS * 128], BF16, name="xb")
-
-        def load_b(cg):
-            rows = x[B_IMAGE].rearrange("c (i d) w -> c d i w", d=2)
-            for di in range(2):
-                nc.sync.dma_start(
-                    out=xb[di:P:2, cg, :].rearrange("p (i w) -> p i w", w=128),
-                    in_=rows[64 * cg : 64 * (cg + 1), di, B_FIRST_ROW : B_FIRST_ROW + B_ROWS, :],
-                )
+        def load_c(hu):
+            xct = xcpool.tile([P, 8, 1024], BF16, name="xct")
+            plane = x[C_IMAGE].rearrange("(cg c) h w -> c cg (h w)", c=32)
+            base = (2 * C_FIRST_ROW + 8 * hu) * 128
+            for s in range(4):
+                d, e = divmod(s, 2)
+                first = base + 128 * d + e
+                nc.sync.dma_start(out=xct[s:P:4, :, 0:C_RUN], in_=plane[:, :, first : first + C_RUN])
+            xc_tiles[hu] = xct
 
         def haar_item(item):
             k, rest = divmod(item, 8)
-            g, q = divmod(rest, 4)
+            hl, rest2 = divmod(rest, 4)
+            g, q = divmod(rest2, 2)
             if rest == 0:
-                gr_tiles[("b", k)] = grbpool.tile([P, 4 * G * 512], BF16, name="grb", align_bytes=64)
+                gr_tiles[("c", k)] = grcpool.tile([P, 4 * G * 512], BF16, name="grc", align_bytes=64)
             hb = auxpool.tile([P, 4, P], F32, name="hb", tag="aux")
-            first = (8 * k + 2 * q) * 128
-            for e in range(2):
-                pair = xb[:, 2 * g + e, first : first + 256].rearrange("p (r c) -> p r c", c=2)
-                for sh in range(2):
-                    t = 2 * e + sh
-                    nc.tensor.matmul(hb[:, t, :], lhsT=sv[:], rhs=pair[:, :, 0], start=True, stop=False)
-                    nc.tensor.matmul(
-                        hb[:, t, :], lhsT=(sv[:] if sh == 0 else svn[:]), rhs=pair[:, :, 1], start=False, stop=True
-                    )
-            c0 = 4 * (512 * g + 128 * q)
-            nc.scalar.activation(
-                out=gr_tiles[("b", k)][:, c0 : c0 + 512].rearrange("p (r t) -> p r t", t=4),
+            for t in range(4):
+                cols = xc_tiles[2 * k + hl][:, 4 * g + t, 512 * q : 512 * (q + 1)].rearrange(
+                    "p (i h j c) -> p i h j c", h=2, j=64, c=2
+                )
+                nc.tensor.matmul(
+                    hb[:, t, :].rearrange("p (i j) -> p i j", j=64),
+                    lhsT=h4[:],
+                    rhs=cols[:, :, 0, :, 0],
+                    start=True,
+                    stop=True,
+                )
+            c0 = 4 * (512 * g + 256 * hl + 128 * q)
+            nc.scalar.copy(
+                out=gr_tiles[("c", k)][:, c0 : c0 + 512].rearrange("p (r t) -> p r t", t=4),
                 in_=hb[:].rearrange("p t r -> p r t"),
-                func=COPY,
-                scale=0.5,
             )
 
         def place(job):
             if job[0] == "a":
                 return A_CHUNKS[job[1]]
-            return (B_IMAGE, 64 * B_FIRST_ROW + 512 * job[1], 512)
+            return (C_IMAGE, 64 * C_FIRST_ROW + 512 * job[1], 512)
 
         def quantise(job):
             npx = place(job)[2]
@@ -186,38 +190,29 @@ def tile_haarwaveletlayer_t_kernel(tc, x, w_fusion, out):
             nc.scalar.dma_start(out=dst[:, :, p0 : p0 + npx], in_=ot[:])
 
         w_sb = const.tile([P, MT * 1024], BF16, name="w_sb")
-        w_sorted = const.tile([P, MT * 1024], BF16, name="w_sorted")
-        w_grouped = {
-            "a": const.tile([P, G * 512 * 4], BF16, name="w_grouped_a", align_bytes=64),
-            "b": const.tile([P, G * 512 * 4], BF16, name="w_grouped_b", align_bytes=64),
-        }
+        w_grouped = {}
         w_quantised = {
             "a": (
                 const.tile([P, G * 512], U32, name="w_codes_a", align_bytes=64),
                 const.tile([P, G * 512], U8, name="w_scales_a", align_bytes=64),
             ),
-            "b": (
-                const.tile([P, G * 512], U32, name="w_codes_b", align_bytes=64),
-                const.tile([P, G * 512], U8, name="w_scales_b", align_bytes=64),
+            "c": (
+                const.tile([P, G * 512], U32, name="w_codes_c", align_bytes=64),
+                const.tile([P, G * 512], U8, name="w_scales_c", align_bytes=64),
             ),
         }
 
-        def sort_w():
-            nc.scalar.copy(
-                out=w_sorted[:].bitcast(F32).rearrange("p (a s q) -> p a s q", s=2, q=128),
-                in_=w_sb[:].bitcast(F32).rearrange("p (a q s) -> p a s q", s=2, q=128),
-            )
-
         def transpose_w_a():
-            ws32 = w_sorted[:].bitcast(F32)
+            w_grouped["a"] = wgpool.tile([P, G * 512 * 4], BF16, name="w_grouped", align_bytes=64)
+            w32 = w_sb[:].bitcast(F32)
             wg32 = w_grouped["a"][:].bitcast(F32)
             for g in range(G):
                 for mp in range(MT // 2):
                     wt = auxpool.tile([P, 2, 2, P], F32, name="wt", tag="aux")
                     for mm in range(2):
-                        for s in range(2):
-                            first = ((2 * (2 * mp + mm) + g) * 2 + s) * 128
-                            nc.tensor.transpose(wt[:, mm, s, :], ws32[:, first : first + 128], ident32[:])
+                        for u in range(2):
+                            first = 512 * (2 * mp + mm) + 256 * g + u
+                            nc.tensor.transpose(wt[:, mm, u, :], w32[:, first : first + 255 : 2], ident32[:])
                     nc.scalar.copy(
                         out=wg32[:, 1024 * g + 512 * mp : 1024 * g + 512 * (mp + 1)].rearrange(
                             "p (m o u) -> p m o u", m=2, u=2
@@ -225,24 +220,22 @@ def tile_haarwaveletlayer_t_kernel(tc, x, w_fusion, out):
                         in_=wt[:].rearrange("p m u o -> p m o u"),
                     )
 
-        def transpose_w_b():
+        def transpose_w_c():
+            w_grouped["c"] = wgpool.tile([P, G * 512 * 4], BF16, name="w_grouped", align_bytes=64)
             for g in range(G):
                 for oh in range(2):
-                    wtb = auxpool.tile([P, 4, 256], BF16, name="wtb", tag="aux")
-                    for e in range(2):
-                        for sh in range(2):
-                            for mm in range(2):
-                                first = (((2 * (2 * oh + mm) + g) * 2 + sh) * 128 + 64 * e) * 2
-                                nc.tensor.transpose(
-                                    wtb[:, 2 * e + sh, P * mm : P * (mm + 1)],
-                                    w_sorted[:, first : first + 128],
-                                    identb[:],
-                                )
+                    wtc = auxpool.tile([P, 4, 256], BF16, name="wtc", tag="aux")
+                    for t in range(4):
+                        for mm in range(2):
+                            first = 1024 * (2 * oh + mm) + 512 * g + 128 * t
+                            nc.tensor.transpose(
+                                wtc[:, t, P * mm : P * (mm + 1)], w_sb[:, first : first + 128], identb[:]
+                            )
                     nc.scalar.copy(
-                        out=w_grouped["b"][:, 2048 * g + 1024 * oh : 2048 * g + 1024 * (oh + 1)].rearrange(
+                        out=w_grouped["c"][:, 2048 * g + 1024 * oh : 2048 * g + 1024 * (oh + 1)].rearrange(
                             "p (o t) -> p o t", t=4
                         ),
-                        in_=wtb[:].rearrange("p t o -> p o t"),
+                        in_=wtc[:].rearrange("p t o -> p o t"),
                     )
 
         def quantise_w(kind):
@@ -262,46 +255,55 @@ def tile_haarwaveletlayer_t_kernel(tc, x, w_fusion, out):
         make_identity(nc, ident32[:])
         identb = const.tile([P, P], BF16, name="identb")
         make_identity(nc, identb[:])
-        sv = const.tile([P, P], BF16, name="sv")
-        svn = const.tile([P, P], BF16, name="svn")
-        idv = identb[:].rearrange("p (c s) -> p c s", s=2)
-        svv = sv[:].rearrange("p (c s) -> p c s", s=2)
-        nc.vector.tensor_tensor(out=svv[:, :, 0], in0=idv[:, :, 0], in1=idv[:, :, 1], op=ADD)
-        nc.vector.tensor_tensor(out=svv[:, :, 1], in0=idv[:, :, 0], in1=idv[:, :, 1], op=SUB)
-        nc.vector.tensor_scalar_mul(out=svn[:], in0=sv[:], scalar1=-1.0)
+        halves = const.tile([P, P], BF16, name="halves")
+        h2 = const.tile([P, P], BF16, name="h2")
+        h4 = const.tile([P, P], BF16, name="h4")
+        nc.vector.tensor_scalar_mul(out=halves[:], in0=identb[:], scalar1=0.5)
+        hv = halves[:].rearrange("p (a e) -> p a e", e=2)
+        h2w = h2[:].rearrange("p (a e) -> p a e", e=2)
+        nc.vector.tensor_tensor(out=h2w[:, :, 0], in0=hv[:, :, 0], in1=hv[:, :, 1], op=ADD)
+        nc.vector.tensor_tensor(out=h2w[:, :, 1], in0=hv[:, :, 0], in1=hv[:, :, 1], op=SUB)
+        h2r = h2[:].rearrange("p (c d h) -> p c d h", d=2, h=2)
+        h4w = h4[:].rearrange("p (c h v) -> p c h v", h=2, v=2)
+        nc.vector.tensor_tensor(out=h4w[:, :, :, 0], in0=h2r[:, :, 0, :], in1=h2r[:, :, 1, :], op=ADD)
+        nc.vector.tensor_tensor(out=h4w[:, :, :, 1], in0=h2r[:, :, 0, :], in1=h2r[:, :, 1, :], op=SUB)
 
         vertical(0)
         load(4)
-        load_b(0)
-        load_b(1)
 
         due = [[] for step in range(NA + 4)]
         item = 0
+        loaded_c = 0
+        quantised_c = 0
         for i in range(NA + 3):
+            finished_c = item // 8
             if i + 1 < NA:
                 vertical(i + 1)
                 if i + 5 < NA:
                     load(i + 5)
-                if i == 0:
-                    load_b(2)
-                    load_b(3)
+            wanted = (sum(C_ITEMS[: i + 3]) + 3) // 4
+            while loaded_c < wanted and loaded_c < item // 4 + 3:
+                load_c(loaded_c)
+                loaded_c += 1
             if i - 1 in REGROUP_ON_VECTOR:
                 regroup(i - 1)
             if i < NA:
                 horizontal(i)
+            if quantised_c < finished_c:
+                quantise(("c", quantised_c))
+                due[max(i + 1, 5)].append(("c", quantised_c))
+                quantised_c += 1
             if 1 <= i <= NA and i - 1 not in REGROUP_ON_VECTOR:
                 regroup(i - 1)
-            if i == 1:
-                sort_w()
             if i == 2:
                 transpose_w_a()
             for job in due[i]:
                 multiply(job)
                 evacuate(job)
             if i == 3:
-                transpose_w_b()
-            if i in B_ITEM_STEPS:
-                for rep in range(B_ITEMS_PER_STEP):
+                transpose_w_c()
+            if i < len(C_ITEMS):
+                for rep in range(C_ITEMS[i]):
                     haar_item(item)
                     item += 1
             if 1 <= i <= NA:
@@ -310,8 +312,4 @@ def tile_haarwaveletlayer_t_kernel(tc, x, w_fusion, out):
             if i == 2:
                 quantise_w("a")
             if i == 4:
-                quantise_w("b")
-            if i in B_QUANTISE_STEP:
-                k = B_QUANTISE_STEP.index(i)
-                quantise(("b", k))
-                due[i + 1].append(("b", k))
+                quantise_w("c")

@@ -49,8 +49,8 @@ def tile_haarwaveletlayer_t_kernel(tc, x, w_fusion, out):
         grcpool = ctx.enter_context(tc.tile_pool(name="grcpool", bufs=2))
         qpool = ctx.enter_context(tc.tile_pool(name="qpool", bufs=4))
         opool = ctx.enter_context(tc.tile_pool(name="opool", bufs=3))
-        accpool = ctx.enter_context(tc.psum_pool(name="accpool", bufs=6))
-        auxpool = ctx.enter_context(tc.psum_pool(name="auxpool", bufs=2))
+        accpool = ctx.enter_context(tc.psum_pool(name="accpool", bufs=5))
+        auxpool = ctx.enter_context(tc.psum_pool(name="auxpool", bufs=3))
         ctx.enter_context(tc.manual_schedule())
 
         x_tiles = {}
@@ -183,7 +183,10 @@ def tile_haarwaveletlayer_t_kernel(tc, x, w_fusion, out):
         def evacuate(job):
             n, p0, npx = place(job)
             per_bank = BANK // npx
-            ot = opool.tile([P, MT, npx], F32, name="ot")
+            if job[0] == "a" and job[1] >= NA - 3:
+                ot = xpool.tile([P, MT, npx], F32, name="xt")
+            else:
+                ot = opool.tile([P, MT, npx], F32, name="ot")
             for b, acc in enumerate(acc_tiles[job]):
                 nc.scalar.copy(out=ot[:, b * per_bank : (b + 1) * per_bank, :], in_=acc[:])
             dst = out[n].rearrange("(m p) i j -> p m (i j)", m=MT)

@@ -71,31 +71,21 @@ def tile_haarwaveletlayer_t_kernel(tc, x, w_fusion, out):
             )
             x_tiles[i] = xt
 
-        def vertical(i):
+        def first_stage(i):
             npx = A_CHUNKS[i][2]
-            xv = x_tiles[i][:].rearrange("p (a d w) -> p a d w", d=2, w=128)
+            xv = x_tiles[i][:].rearrange("p (r e) -> p r e", e=2)
             tt = tpool.tile([P, 2, G * 2 * npx], F32, name="tt")
-            for v, op in ((0, ADD), (1, SUB)):
-                nc.vector.tensor_tensor(
-                    out=tt[:, v, :].rearrange("p (a w) -> p a w", w=128),
-                    in0=xv[:, :, 0, :],
-                    in1=xv[:, :, 1, :],
-                    op=op,
-                )
+            for h, op in ((0, ADD), (1, SUB)):
+                nc.vector.tensor_tensor(out=tt[:, h, :], in0=xv[:, :, 0], in1=xv[:, :, 1], op=op)
             t_tiles[i] = tt
 
-        def horizontal(i):
+        def second_stage(i):
             npx = A_CHUNKS[i][2]
-            half = 2 * G * npx
-            tv = t_tiles[i][:].rearrange("p v (r e) -> p (v r) e", e=2)
-            pl = plpool.tile([P, 2 * half], BF16, name="pl")
-            for h, op in ((0, ADD), (1, SUB)):
-                nc.vector.tensor_tensor(
-                    out=pl[:, half * h : half * (h + 1)],
-                    in0=tv[:, :, 0],
-                    in1=tv[:, :, 1],
-                    op=op,
-                )
+            tv = t_tiles[i][:].rearrange("p h (a d j) -> p h a d j", d=2, j=64)
+            pl = plpool.tile([P, 4 * G * npx], BF16, name="pl")
+            plv = pl[:].rearrange("p (h v a j) -> p v h a j", h=2, v=2, j=64)
+            for v, op in ((0, ADD), (1, SUB)):
+                nc.vector.tensor_tensor(out=plv[:, v], in0=tv[:, :, :, 0, :], in1=tv[:, :, :, 1, :], op=op)
             pl_tiles[i] = pl
 
         def regroup(i):
@@ -271,7 +261,7 @@ def tile_haarwaveletlayer_t_kernel(tc, x, w_fusion, out):
         nc.vector.tensor_tensor(out=h4w[:, :, :, 0], in0=h2r[:, :, 0, :], in1=h2r[:, :, 1, :], op=ADD)
         nc.vector.tensor_tensor(out=h4w[:, :, :, 1], in0=h2r[:, :, 0, :], in1=h2r[:, :, 1, :], op=SUB)
 
-        vertical(0)
+        first_stage(0)
         load(4)
 
         due = [[] for step in range(NA + 4)]
@@ -281,7 +271,7 @@ def tile_haarwaveletlayer_t_kernel(tc, x, w_fusion, out):
         for i in range(NA + 3):
             finished_c = item // 8
             if i + 1 < NA:
-                vertical(i + 1)
+                first_stage(i + 1)
                 if i + 5 < NA:
                     load(i + 5)
             wanted = (sum(C_ITEMS[: i + 3]) + 3) // 4
@@ -291,7 +281,7 @@ def tile_haarwaveletlayer_t_kernel(tc, x, w_fusion, out):
             if i - 1 in REGROUP_ON_VECTOR:
                 regroup(i - 1)
             if i < NA:
-                horizontal(i)
+                second_stage(i)
             if quantised_c < finished_c:
                 quantise(("c", quantised_c))
                 due[max(i + 1, 5)].append(("c", quantised_c))

@@ -22,7 +22,7 @@ BANK = 512
 N_C = 6
 C_IMAGE = 1
 C_FIRST_ROW = 64 - 8 * N_C
-C_ITEMS = (0, 0, 4, 5, 5, 5, 5, 5, 5, 5, 5, 4)
+C_ITEMS = (0, 0, 2, 2, 3, 2, 3, 2, 3, 2, 3, 2)
 C_RUN = 895
 LAST_A = 512 * (7 - N_C)
 A_CHUNKS = (
@@ -32,8 +32,8 @@ A_CHUNKS = (
     + [(1, LAST_A, 256), (1, LAST_A + 256, 128), (1, LAST_A + 384, 128)]
 )
 NA = len(A_CHUNKS)
-assert sum(C_ITEMS) == 8 * N_C
-REGROUP_ON_VECTOR = tuple(range(NA - 5, NA))
+assert sum(C_ITEMS) == 4 * N_C
+REGROUP_ON_VECTOR = tuple(range(NA - 3, NA))
 
 
 def tile_haarwaveletlayer_t_kernel(tc, x, w_fusion, out):
@@ -110,27 +110,26 @@ def tile_haarwaveletlayer_t_kernel(tc, x, w_fusion, out):
             xc_tiles[hu] = xct
 
         def haar_item(item):
-            k, rest = divmod(item, 8)
-            hl, rest2 = divmod(rest, 4)
-            g, q = divmod(rest2, 2)
+            k, rest = divmod(item, 4)
+            hl, g = divmod(rest, 2)
             if rest == 0:
                 gr_tiles[("c", k)] = grcpool.tile([P, 4 * G * 512], BF16, name="grc", align_bytes=64)
-            hb = auxpool.tile([P, 4, P], F32, name="hb", tag="aux")
-            for t in range(4):
-                cols = xc_tiles[2 * k + hl][:, 4 * g + t, 512 * q : 512 * (q + 1)].rearrange(
-                    "p (i h j c) -> p i h j c", h=2, j=64, c=2
+            hb = auxpool.tile([P, 2, 512], BF16, name="hb", tag="aux")
+            for q in range(2):
+                cols = xc_tiles[2 * k + hl][:, 4 * g : 4 * (g + 1), 512 * q : 512 * (q + 1)].rearrange(
+                    "p t (i h j c) -> p i j t h c", h=2, j=64, c=2
                 )
                 nc.tensor.matmul(
-                    hb[:, t, :].rearrange("p (i j) -> p i j", j=64),
+                    hb[:, q, :].rearrange("p (i j t) -> p i j t", j=64, t=4),
                     lhsT=h4[:],
-                    rhs=cols[:, :, 0, :, 0],
+                    rhs=cols[:, :, :, :, 0, 0],
                     start=True,
                     stop=True,
                 )
-            c0 = 4 * (512 * g + 256 * hl + 128 * q)
+            c0 = 4 * (512 * g + 256 * hl)
             nc.scalar.copy(
-                out=gr_tiles[("c", k)][:, c0 : c0 + 512].rearrange("p (r t) -> p r t", t=4),
-                in_=hb[:].rearrange("p t r -> p r t"),
+                out=gr_tiles[("c", k)][:, c0 : c0 + 1024],
+                in_=hb[:].rearrange("p q f -> p (q f)"),
             )
 
         def place(job):
@@ -269,13 +268,13 @@ def tile_haarwaveletlayer_t_kernel(tc, x, w_fusion, out):
         loaded_c = 0
         quantised_c = 0
         for i in range(NA + 3):
-            finished_c = item // 8
+            finished_c = item // 4
             if i + 1 < NA:
                 first_stage(i + 1)
                 if i + 5 < NA:
                     load(i + 5)
-            wanted = (sum(C_ITEMS[: i + 3]) + 3) // 4
-            while loaded_c < wanted and loaded_c < item // 4 + 3:
+            wanted = (sum(C_ITEMS[: i + 3]) + 1) // 2
+            while loaded_c < wanted and loaded_c < item // 2 + 3:
                 load_c(loaded_c)
                 loaded_c += 1
             if i - 1 in REGROUP_ON_VECTOR:

@@ -33,7 +33,6 @@ A_CHUNKS = (
 )
 NA = len(A_CHUNKS)
 assert sum(C_ITEMS) == 4 * N_C
-REGROUP_ON_VECTOR = tuple(range(NA - 3, NA))
 
 
 def tile_haarwaveletlayer_t_kernel(tc, x, w_fusion, out):
@@ -44,7 +43,6 @@ def tile_haarwaveletlayer_t_kernel(tc, x, w_fusion, out):
         xpool = ctx.enter_context(tc.tile_pool(name="xpool", bufs=4))
         xcpool = ctx.enter_context(tc.tile_pool(name="xcpool", bufs=3))
         tpool = ctx.enter_context(tc.tile_pool(name="tpool", bufs=2))
-        plpool = ctx.enter_context(tc.tile_pool(name="plpool", bufs=2))
         grpool = ctx.enter_context(tc.tile_pool(name="grpool", bufs=2))
         grcpool = ctx.enter_context(tc.tile_pool(name="grcpool", bufs=2))
         qpool = ctx.enter_context(tc.tile_pool(name="qpool", bufs=4))
@@ -56,7 +54,6 @@ def tile_haarwaveletlayer_t_kernel(tc, x, w_fusion, out):
         x_tiles = {}
         xc_tiles = {}
         t_tiles = {}
-        pl_tiles = {}
         gr_tiles = {}
         q_tiles = {}
         acc_tiles = {}
@@ -73,30 +70,27 @@ def tile_haarwaveletlayer_t_kernel(tc, x, w_fusion, out):
 
         def first_stage(i):
             npx = A_CHUNKS[i][2]
-            xv = x_tiles[i][:].rearrange("p (r e) -> p r e", e=2)
-            tt = tpool.tile([P, 2, G * 2 * npx], F32, name="tt")
-            for h, op in ((0, ADD), (1, SUB)):
-                nc.vector.tensor_tensor(out=tt[:, h, :], in0=xv[:, :, 0], in1=xv[:, :, 1], op=op)
+            xv = x_tiles[i][:].rearrange("p (a d j e) -> p d e a j", d=2, j=64, e=2)
+            tt = tpool.tile([P, 6, G * npx], F32, name="tt")
+            tv = tt[:].rearrange("p (e v) (a j) -> p v e a j", v=2, j=64)
+            for v, op in ((0, ADD), (1, SUB)):
+                nc.vector.tensor_tensor(out=tv[:, v, 0:2], in0=xv[:, 0], in1=xv[:, 1], op=op)
             t_tiles[i] = tt
+
+        def negate(i):
+            tt = t_tiles[i]
+            nc.scalar.activation(out=tt[:, 4:6, :], in_=tt[:, 0:2, :], func=COPY, scale=-1.0)
 
         def second_stage(i):
             npx = A_CHUNKS[i][2]
-            tv = t_tiles[i][:].rearrange("p h (a d j) -> p h a d j", d=2, j=64)
-            pl = plpool.tile([P, 4 * G * npx], BF16, name="pl")
-            plv = pl[:].rearrange("p (h v a j) -> p v h a j", h=2, v=2, j=64)
-            for v, op in ((0, ADD), (1, SUB)):
-                nc.vector.tensor_tensor(out=plv[:, v], in0=tv[:, :, :, 0, :], in1=tv[:, :, :, 1, :], op=op)
-            pl_tiles[i] = pl
-
-        def regroup(i):
-            npx = A_CHUNKS[i][2]
             gr = grpool.tile([P, 4 * G * npx], BF16, name="gr", align_bytes=64)
-            dst = gr[:].rearrange("p (c i t) -> p c t i", i=4, t=4)
-            src = pl_tiles[i][:].rearrange("p (t c i) -> p c t i", t=4, i=4)
-            if i in REGROUP_ON_VECTOR:
-                nc.vector.tensor_scalar_mul(out=dst, in0=src, scalar1=0.5)
-            else:
-                nc.scalar.activation(out=dst, in_=src, func=COPY, scale=0.5)
+            tv = t_tiles[i][:].rearrange("p t (c i) -> p c t i", i=4)
+            nc.vector.tensor_tensor(
+                out=gr[:].rearrange("p (c i t) -> p c t i", i=4, t=4),
+                in0=tv[:, :, 0:4, :],
+                in1=tv[:, :, 2:6, :],
+                op=SUB,
+            )
             gr_tiles[("a", i)] = gr
 
         def load_c(hu):
@@ -177,7 +171,11 @@ def tile_haarwaveletlayer_t_kernel(tc, x, w_fusion, out):
             else:
                 ot = opool.tile([P, MT, npx], F32, name="ot")
             for b, acc in enumerate(acc_tiles[job]):
-                nc.scalar.copy(out=ot[:, b * per_bank : (b + 1) * per_bank, :], in_=acc[:])
+                dst_ot = ot[:, b * per_bank : (b + 1) * per_bank, :]
+                if job[0] == "a":
+                    nc.scalar.activation(out=dst_ot, in_=acc[:], func=COPY, scale=0.5)
+                else:
+                    nc.scalar.copy(out=dst_ot, in_=acc[:])
             dst = out[n].rearrange("(m p) i j -> p m (i j)", m=MT)
             nc.scalar.dma_start(out=dst[:, :, p0 : p0 + npx], in_=ot[:])
 
@@ -204,7 +202,7 @@ def tile_haarwaveletlayer_t_kernel(tc, x, w_fusion, out):
                     for mm in range(2):
                         for u in range(2):
                             first = 512 * (2 * mp + mm) + 256 * g + u
-                            nc.tensor.transpose(wt[:, mm, u, :], w32[:, first : first + 255 : 2], ident32[:])
+                            nc.tensor.transpose(wt[:, mm, 1 - u, :], w32[:, first : first + 255 : 2], ident32[:])
                     nc.scalar.copy(
                         out=wg32[:, 1024 * g + 512 * mp : 1024 * g + 512 * (mp + 1)].rearrange(
                             "p (m o u) -> p m o u", m=2, u=2
@@ -261,6 +259,7 @@ def tile_haarwaveletlayer_t_kernel(tc, x, w_fusion, out):
         nc.vector.tensor_tensor(out=h4w[:, :, :, 1], in0=h2r[:, :, 0, :], in1=h2r[:, :, 1, :], op=SUB)
 
         first_stage(0)
+        negate(0)
         load(4)
 
         due = [[] for step in range(NA + 4)]
@@ -277,16 +276,12 @@ def tile_haarwaveletlayer_t_kernel(tc, x, w_fusion, out):
             while loaded_c < wanted and loaded_c < item // 2 + 3:
                 load_c(loaded_c)
                 loaded_c += 1
-            if i - 1 in REGROUP_ON_VECTOR:
-                regroup(i - 1)
             if i < NA:
                 second_stage(i)
             if quantised_c < finished_c:
                 quantise(("c", quantised_c))
                 due[max(i + 1, 5)].append(("c", quantised_c))
                 quantised_c += 1
-            if 1 <= i <= NA and i - 1 not in REGROUP_ON_VECTOR:
-                regroup(i - 1)
             if i == 2:
                 transpose_w_a()
             for job in due[i]:
@@ -298,6 +293,8 @@ def tile_haarwaveletlayer_t_kernel(tc, x, w_fusion, out):
                 for rep in range(C_ITEMS[i]):
                     haar_item(item)
                     item += 1
+            if i + 1 < NA:
+                negate(i + 1)
             if 1 <= i <= NA:
                 quantise(("a", i - 1))
                 due[max(i + 1, 3)].append(("a", i - 1))

@@ -21,9 +21,9 @@ BANK = 512
 
 N_C = 6
 C_IMAGE = 1
-C_FIRST_ROW = 64 - 8 * N_C
-C_ITEMS = (0, 0, 2, 2, 3, 2, 3, 2, 3, 2, 3, 2)
-C_RUN = 895
+C_FIRST = 4096 - 512 * N_C
+C_SLOTS = (0, 2, 3, 3, 3, 3, 3, 3, 3, 3)
+C_ITEMS = 4 * N_C
 LAST_A = 512 * (7 - N_C)
 A_CHUNKS = (
     [(0, 0, 128), (0, 128, 128), (0, 256, 256)]
@@ -32,7 +32,7 @@ A_CHUNKS = (
     + [(1, LAST_A, 256), (1, LAST_A + 256, 128), (1, LAST_A + 384, 128)]
 )
 NA = len(A_CHUNKS)
-assert sum(C_ITEMS) == 4 * N_C
+assert sum(C_SLOTS) == C_ITEMS + 2
 
 
 def tile_haarwaveletlayer_t_kernel(tc, x, w_fusion, out):
@@ -42,35 +42,47 @@ def tile_haarwaveletlayer_t_kernel(tc, x, w_fusion, out):
         wgpool = ctx.enter_context(tc.tile_pool(name="wgpool", bufs=1))
         xpool = ctx.enter_context(tc.tile_pool(name="xpool", bufs=4))
         xcpool = ctx.enter_context(tc.tile_pool(name="xcpool", bufs=3))
+        xrpool = ctx.enter_context(tc.tile_pool(name="xrpool", bufs=3))
+        xtpool = ctx.enter_context(tc.tile_pool(name="xtpool", bufs=3))
         tpool = ctx.enter_context(tc.tile_pool(name="tpool", bufs=2))
         grpool = ctx.enter_context(tc.tile_pool(name="grpool", bufs=2))
         grcpool = ctx.enter_context(tc.tile_pool(name="grcpool", bufs=2))
         qpool = ctx.enter_context(tc.tile_pool(name="qpool", bufs=4))
         opool = ctx.enter_context(tc.tile_pool(name="opool", bufs=3))
-        accpool = ctx.enter_context(tc.psum_pool(name="accpool", bufs=5))
-        auxpool = ctx.enter_context(tc.psum_pool(name="auxpool", bufs=3))
+        accpool = ctx.enter_context(tc.psum_pool(name="accpool", bufs=4))
+        turnpool = ctx.enter_context(tc.psum_pool(name="turnpool", bufs=2))
+        bandpool = ctx.enter_context(tc.psum_pool(name="bandpool", bufs=2))
         ctx.enter_context(tc.manual_schedule())
 
         x_tiles = {}
-        xc_tiles = {}
+        xr_tiles = {}
+        turn_tiles = {}
+        turned_tiles = {}
+        band_tiles = {}
         t_tiles = {}
         gr_tiles = {}
         q_tiles = {}
         acc_tiles = {}
 
-        def load(i):
-            n, p0, npx = A_CHUNKS[i]
-            xt = xpool.tile([P, G * 4 * npx], BF16, name="xt")
+        def place(job):
+            if job[0] == "a":
+                return A_CHUNKS[job[1]]
+            return (C_IMAGE, C_FIRST + 512 * job[1], 512)
+
+        def load(job):
+            n, p0, npx = place(job)
+            pool = xpool if job[0] == "a" else xcpool
+            xt = pool.tile([P, G * 4 * npx], BF16, name="xt")
             src = x[n].rearrange("(g p) h w -> p g (h w)", g=G)
             nc.sync.dma_start(
                 out=xt[:].rearrange("p (g f) -> p g f", g=G),
                 in_=src[:, :, 4 * p0 : 4 * (p0 + npx)],
             )
-            x_tiles[i] = xt
+            x_tiles[job] = xt
 
         def first_stage(i):
             npx = A_CHUNKS[i][2]
-            xv = x_tiles[i][:].rearrange("p (a d j e) -> p d e a j", d=2, j=64, e=2)
+            xv = x_tiles[("a", i)][:].rearrange("p (a d j e) -> p d e a j", d=2, j=64, e=2)
             tt = tpool.tile([P, 6, G * npx], F32, name="tt")
             tv = tt[:].rearrange("p (e v) (a j) -> p v e a j", v=2, j=64)
             for v, op in ((0, ADD), (1, SUB)):
@@ -93,43 +105,41 @@ def tile_haarwaveletlayer_t_kernel(tc, x, w_fusion, out):
             )
             gr_tiles[("a", i)] = gr
 
-        def load_c(hu):
-            xct = xcpool.tile([P, 8, 1024], BF16, name="xct")
-            plane = x[C_IMAGE].rearrange("(cg c) h w -> c cg (h w)", c=32)
-            base = (2 * C_FIRST_ROW + 8 * hu) * 128
-            for s in range(4):
-                d, e = divmod(s, 2)
-                first = base + 128 * d + e
-                nc.sync.dma_start(out=xct[s:P:4, :, 0:C_RUN], in_=plane[:, :, first : first + C_RUN])
-            xc_tiles[hu] = xct
+        def split_rows(k, g):
+            xr = xrpool.tile([P, 2, 8, P], BF16, name="xr")
+            src = x_tiles[("c", k)][:, 2048 * g : 2048 * (g + 1)].rearrange("p (r h c) -> p h r c", h=2, c=64)
+            nc.scalar.copy(out=xr[:].rearrange("p h a (d c) -> p h (a d) c", d=2), in_=src)
+            xr_tiles[(k, g)] = xr
 
-        def haar_item(item):
-            k, rest = divmod(item, 4)
-            hl, g = divmod(rest, 2)
-            if rest == 0:
+        def turn(item):
+            k, g, q = item // 4, item // 2 % 2, item % 2
+            if q == 0:
+                split_rows(k, g)
+            tb = turnpool.tile([P, 8, P], BF16, name="tb")
+            for b in range(8):
+                a, h = 4 * q + b // 2, b % 2
+                nc.tensor.transpose(tb[:, b, :], xr_tiles[(k, g)][:, h, a, :], identb[:])
+            turn_tiles[item] = tb
+
+        def take_turned(item):
+            xt = xtpool.tile([P, 8, P], BF16, name="xturned")
+            nc.scalar.copy(out=xt[:], in_=turn_tiles[item][:])
+            turned_tiles[item] = xt
+
+        def make_bands(item):
+            bb = bandpool.tile([P, 8, P], BF16, name="bb")
+            for b in range(8):
+                nc.tensor.matmul(bb[:, b, :], lhsT=turned_tiles[item][:, b, :], rhs=haar[:], start=True, stop=True)
+            band_tiles[item] = bb
+
+        def take_bands(item):
+            k, gq = divmod(item, 4)
+            if gq == 0:
                 gr_tiles[("c", k)] = grcpool.tile([P, 4 * G * 512], BF16, name="grc", align_bytes=64)
-            hb = auxpool.tile([P, 2, 512], BF16, name="hb", tag="aux")
-            for q in range(2):
-                cols = xc_tiles[2 * k + hl][:, 4 * g : 4 * (g + 1), 512 * q : 512 * (q + 1)].rearrange(
-                    "p t (i h j c) -> p i j t h c", h=2, j=64, c=2
-                )
-                nc.tensor.matmul(
-                    hb[:, q, :].rearrange("p (i j t) -> p i j t", j=64, t=4),
-                    lhsT=h4[:],
-                    rhs=cols[:, :, :, :, 0, 0],
-                    start=True,
-                    stop=True,
-                )
-            c0 = 4 * (512 * g + 256 * hl)
             nc.scalar.copy(
-                out=gr_tiles[("c", k)][:, c0 : c0 + 1024],
-                in_=hb[:].rearrange("p q f -> p (q f)"),
+                out=gr_tiles[("c", k)][:, 1024 * gq : 1024 * (gq + 1)],
+                in_=band_tiles[item][:].rearrange("p b f -> p (b f)"),
             )
-
-        def place(job):
-            if job[0] == "a":
-                return A_CHUNKS[job[1]]
-            return (C_IMAGE, 64 * C_FIRST_ROW + 512 * job[1], 512)
 
         def quantise(job):
             npx = place(job)[2]
@@ -141,7 +151,6 @@ def tile_haarwaveletlayer_t_kernel(tc, x, w_fusion, out):
         def multiply(job):
             npx = place(job)[2]
             codes, scales = q_tiles[job]
-            wc, ws = w_quantised[job[0]]
             per_bank = BANK // npx
             banks = []
             for b in range(MT // per_bank):
@@ -153,8 +162,8 @@ def tile_haarwaveletlayer_t_kernel(tc, x, w_fusion, out):
                         xcols = slice(npx * g, npx * (g + 1))
                         nc.tensor.matmul_mx(
                             out=acc[:, s, :],
-                            lhsT=wc[:, wcols].bitcast(FP8X4),
-                            lhsT_scale=ws[:, wcols],
+                            lhsT=w_codes[:, wcols].bitcast(FP8X4),
+                            lhsT_scale=w_scales[:, wcols],
                             rhs=codes[:, xcols].bitcast(FP8X4),
                             rhs_scale=scales[:, xcols],
                             start=(g == 0),
@@ -171,34 +180,23 @@ def tile_haarwaveletlayer_t_kernel(tc, x, w_fusion, out):
             else:
                 ot = opool.tile([P, MT, npx], F32, name="ot")
             for b, acc in enumerate(acc_tiles[job]):
-                dst_ot = ot[:, b * per_bank : (b + 1) * per_bank, :]
-                if job[0] == "a":
-                    nc.scalar.activation(out=dst_ot, in_=acc[:], func=COPY, scale=0.5)
-                else:
-                    nc.scalar.copy(out=dst_ot, in_=acc[:])
+                nc.scalar.activation(
+                    out=ot[:, b * per_bank : (b + 1) * per_bank, :], in_=acc[:], func=COPY, scale=0.5
+                )
             dst = out[n].rearrange("(m p) i j -> p m (i j)", m=MT)
             nc.scalar.dma_start(out=dst[:, :, p0 : p0 + npx], in_=ot[:])
 
         w_sb = const.tile([P, MT * 1024], BF16, name="w_sb")
-        w_grouped = {}
-        w_quantised = {
-            "a": (
-                const.tile([P, G * 512], U32, name="w_codes_a", align_bytes=64),
-                const.tile([P, G * 512], U8, name="w_scales_a", align_bytes=64),
-            ),
-            "c": (
-                const.tile([P, G * 512], U32, name="w_codes_c", align_bytes=64),
-                const.tile([P, G * 512], U8, name="w_scales_c", align_bytes=64),
-            ),
-        }
+        w_grouped = wgpool.tile([P, G * 512 * 4], BF16, name="w_grouped", align_bytes=64)
+        w_codes = const.tile([P, G * 512], U32, name="w_codes", align_bytes=64)
+        w_scales = const.tile([P, G * 512], U8, name="w_scales", align_bytes=64)
 
-        def transpose_w_a():
-            w_grouped["a"] = wgpool.tile([P, G * 512 * 4], BF16, name="w_grouped", align_bytes=64)
+        def transpose_w():
             w32 = w_sb[:].bitcast(F32)
-            wg32 = w_grouped["a"][:].bitcast(F32)
+            wg32 = w_grouped[:].bitcast(F32)
             for g in range(G):
                 for mp in range(MT // 2):
-                    wt = auxpool.tile([P, 2, 2, P], F32, name="wt", tag="aux")
+                    wt = accpool.tile([P, 2, 2, P], F32, name="wt", tag="acc")
                     for mm in range(2):
                         for u in range(2):
                             first = 512 * (2 * mp + mm) + 256 * g + u
@@ -210,95 +208,73 @@ def tile_haarwaveletlayer_t_kernel(tc, x, w_fusion, out):
                         in_=wt[:].rearrange("p m u o -> p m o u"),
                     )
 
-        def transpose_w_c():
-            w_grouped["c"] = wgpool.tile([P, G * 512 * 4], BF16, name="w_grouped", align_bytes=64)
-            for g in range(G):
-                for oh in range(2):
-                    wtc = auxpool.tile([P, 4, 256], BF16, name="wtc", tag="aux")
-                    for t in range(4):
-                        for mm in range(2):
-                            first = 1024 * (2 * oh + mm) + 512 * g + 128 * t
-                            nc.tensor.transpose(
-                                wtc[:, t, P * mm : P * (mm + 1)], w_sb[:, first : first + 128], identb[:]
-                            )
-                    nc.scalar.copy(
-                        out=w_grouped["c"][:, 2048 * g + 1024 * oh : 2048 * g + 1024 * (oh + 1)].rearrange(
-                            "p (o t) -> p o t", t=4
-                        ),
-                        in_=wtc[:].rearrange("p t o -> p o t"),
-                    )
-
-        def quantise_w(kind):
-            wc, ws = w_quantised[kind]
-            nc.vector.quantize_mx(out=wc[:].bitcast(FP8X4), scales=ws[:], in_=w_grouped[kind][:])
-
-        load(0)
-        load(1)
-        load(2)
+        load(("a", 0))
+        load(("a", 1))
+        load(("a", 2))
         nc.sync.dma_start(
             out=w_sb[:].rearrange("p (m k) -> p m k", m=MT),
             in_=w_fusion.rearrange("(m p) k a b -> p m (k a b)", m=MT),
         )
-        load(3)
+        load(("c", 0))
+        load(("a", 3))
 
         ident32 = const.tile([P, P], F32, name="ident32")
         make_identity(nc, ident32[:])
         identb = const.tile([P, P], BF16, name="identb")
         make_identity(nc, identb[:])
-        halves = const.tile([P, P], BF16, name="halves")
-        h2 = const.tile([P, P], BF16, name="h2")
-        h4 = const.tile([P, P], BF16, name="h4")
-        nc.vector.tensor_scalar_mul(out=halves[:], in0=identb[:], scalar1=0.5)
-        hv = halves[:].rearrange("p (a e) -> p a e", e=2)
-        h2w = h2[:].rearrange("p (a e) -> p a e", e=2)
-        nc.vector.tensor_tensor(out=h2w[:, :, 0], in0=hv[:, :, 0], in1=hv[:, :, 1], op=ADD)
-        nc.vector.tensor_tensor(out=h2w[:, :, 1], in0=hv[:, :, 0], in1=hv[:, :, 1], op=SUB)
-        h2r = h2[:].rearrange("p (c d h) -> p c d h", d=2, h=2)
-        h4w = h4[:].rearrange("p (c h v) -> p c h v", h=2, v=2)
-        nc.vector.tensor_tensor(out=h4w[:, :, :, 0], in0=h2r[:, :, 0, :], in1=h2r[:, :, 1, :], op=ADD)
-        nc.vector.tensor_tensor(out=h4w[:, :, :, 1], in0=h2r[:, :, 0, :], in1=h2r[:, :, 1, :], op=SUB)
+        h2 = const.tile([P, 2, 32, 2], BF16, name="h2")
+        haar = const.tile([P, P], BF16, name="haar")
+        iv = identb[:].rearrange("p (d j e) -> p d j e", d=2, e=2)
+        nc.vector.tensor_tensor(out=h2[:, :, :, 0], in0=iv[:, :, :, 0], in1=iv[:, :, :, 1], op=ADD)
+        nc.vector.tensor_tensor(out=h2[:, :, :, 1], in0=iv[:, :, :, 0], in1=iv[:, :, :, 1], op=SUB)
+        hw = haar[:].rearrange("p (j h v) -> p j h v", h=2, v=2)
+        for h in range(2):
+            for v, op in ((0, ADD), (1, SUB)):
+                nc.vector.tensor_tensor(out=hw[:, :, 1 - h, v], in0=h2[:, 0, :, h], in1=h2[:, 1, :, h], op=op)
 
         first_stage(0)
         negate(0)
-        load(4)
+        load(("a", 4))
+        load(("c", 1))
 
         due = [[] for step in range(NA + 4)]
-        item = 0
-        loaded_c = 0
+        slot = 0
+        loaded_c = 2
         quantised_c = 0
         for i in range(NA + 3):
-            finished_c = item // 4
+            finished_c = max(slot - 2, 0) // 4
             if i + 1 < NA:
                 first_stage(i + 1)
                 if i + 5 < NA:
-                    load(i + 5)
-            wanted = (sum(C_ITEMS[: i + 3]) + 1) // 2
-            while loaded_c < wanted and loaded_c < item // 2 + 3:
-                load_c(loaded_c)
+                    load(("a", i + 5))
+            while loaded_c < N_C and loaded_c < slot // 4 + 3:
+                load(("c", loaded_c))
                 loaded_c += 1
             if i < NA:
                 second_stage(i)
             if quantised_c < finished_c:
                 quantise(("c", quantised_c))
-                due[max(i + 1, 5)].append(("c", quantised_c))
+                due[max(i + 1, 3)].append(("c", quantised_c))
                 quantised_c += 1
             if i == 2:
-                transpose_w_a()
+                transpose_w()
             for job in due[i]:
                 multiply(job)
                 evacuate(job)
-            if i == 3:
-                transpose_w_c()
-            if i < len(C_ITEMS):
-                for rep in range(C_ITEMS[i]):
-                    haar_item(item)
-                    item += 1
             if i + 1 < NA:
                 negate(i + 1)
+            if i < len(C_SLOTS):
+                for rep in range(C_SLOTS[i]):
+                    if slot < C_ITEMS:
+                        turn(slot)
+                    if 0 <= slot - 1 < C_ITEMS:
+                        take_turned(slot - 1)
+                        make_bands(slot - 1)
+                    if 0 <= slot - 2:
+                        take_bands(slot - 2)
+                    slot += 1
             if 1 <= i <= NA:
                 quantise(("a", i - 1))
                 due[max(i + 1, 3)].append(("a", i - 1))
             if i == 2:
-                quantise_w("a")
-            if i == 4:
-                quantise_w("c")
+                nc.vector.quantize_mx(out=w_codes[:].bitcast(FP8X4), scales=w_scales[:], in_=w_grouped[:])

@@ -15,7 +15,6 @@ SUB = mybir.AluOpType.subtract
 COPY = mybir.ActivationFunctionType.Copy
 
 P = 128
-G = 2
 MT = 4
 BANK = 512
 
@@ -32,6 +31,7 @@ A_CHUNKS = (
     + [(1, LAST_A, 256), (1, LAST_A + 256, 128), (1, LAST_A + 384, 128)]
 )
 NA = len(A_CHUNKS)
+EVAC_LAG = 2
 assert sum(C_SLOTS) == C_ITEMS + 2
 
 
@@ -39,16 +39,15 @@ def tile_haarwaveletlayer_t_kernel(tc, x, w_fusion, out):
     nc = tc.nc
     with ExitStack() as ctx:
         const = ctx.enter_context(tc.tile_pool(name="const", bufs=1))
-        wgpool = ctx.enter_context(tc.tile_pool(name="wgpool", bufs=1))
         xpool = ctx.enter_context(tc.tile_pool(name="xpool", bufs=4))
         xcpool = ctx.enter_context(tc.tile_pool(name="xcpool", bufs=3))
-        xrpool = ctx.enter_context(tc.tile_pool(name="xrpool", bufs=3))
+        xrpool = ctx.enter_context(tc.tile_pool(name="xrpool", bufs=2))
         xtpool = ctx.enter_context(tc.tile_pool(name="xtpool", bufs=3))
         tpool = ctx.enter_context(tc.tile_pool(name="tpool", bufs=2))
         grpool = ctx.enter_context(tc.tile_pool(name="grpool", bufs=2))
         grcpool = ctx.enter_context(tc.tile_pool(name="grcpool", bufs=2))
         qpool = ctx.enter_context(tc.tile_pool(name="qpool", bufs=4))
-        opool = ctx.enter_context(tc.tile_pool(name="opool", bufs=3))
+        opool = ctx.enter_context(tc.tile_pool(name="opool", bufs=4))
         accpool = ctx.enter_context(tc.psum_pool(name="accpool", bufs=4))
         turnpool = ctx.enter_context(tc.psum_pool(name="turnpool", bufs=2))
         bandpool = ctx.enter_context(tc.psum_pool(name="bandpool", bufs=2))
@@ -62,180 +61,195 @@ def tile_haarwaveletlayer_t_kernel(tc, x, w_fusion, out):
         t_tiles = {}
         gr_tiles = {}
         q_tiles = {}
-        acc_tiles = {}
+        out_tiles = {}
+        filled = []
 
         def place(job):
             if job[0] == "a":
                 return A_CHUNKS[job[1]]
             return (C_IMAGE, C_FIRST + 512 * job[1], 512)
 
-        def load(job):
+        def load(job, queues):
             n, p0, npx = place(job)
             pool = xpool if job[0] == "a" else xcpool
-            xt = pool.tile([P, G * 4 * npx], BF16, name="xt")
-            src = x[n].rearrange("(g p) h w -> p g (h w)", g=G)
-            nc.sync.dma_start(
-                out=xt[:].rearrange("p (g f) -> p g f", g=G),
-                in_=src[:, :, 4 * p0 : 4 * (p0 + npx)],
-            )
+            xt = pool.tile([P, 2, 4 * npx], BF16, name="xt")
+            src = x[n].rearrange("(s u r) h w -> s r u (h w)", s=4, u=2)
+            for s in range(4):
+                queues[s // 2].dma_start(
+                    out=xt[32 * s : 32 * (s + 1), :, :], in_=src[s, :, :, 4 * p0 : 4 * (p0 + npx)]
+                )
             x_tiles[job] = xt
 
         def first_stage(i):
             npx = A_CHUNKS[i][2]
-            xv = x_tiles[("a", i)][:].rearrange("p (a d j e) -> p d e a j", d=2, j=64, e=2)
-            tt = tpool.tile([P, 6, G * npx], F32, name="tt")
-            tv = tt[:].rearrange("p (e v) (a j) -> p v e a j", v=2, j=64)
-            for v, op in ((0, ADD), (1, SUB)):
-                nc.vector.tensor_tensor(out=tv[:, v, 0:2], in0=xv[:, 0], in1=xv[:, 1], op=op)
+            xv = x_tiles[("a", i)][:].rearrange("p u (a d j e) -> p d u a j e", d=2, j=64, e=2)
+            tt = tpool.tile([P, 2, 2, 2, npx], F32, name="tt")
+            tv = tt[:].rearrange("p d u h (a j) -> p h d u a j", j=64)
+            for h, op in ((0, ADD), (1, SUB)):
+                nc.vector.tensor_tensor(
+                    out=tv[:, h], in0=xv[:, :, :, :, :, 0], in1=xv[:, :, :, :, :, 1], op=op
+                )
             t_tiles[i] = tt
-
-        def negate(i):
-            tt = t_tiles[i]
-            nc.scalar.activation(out=tt[:, 4:6, :], in_=tt[:, 0:2, :], func=COPY, scale=-1.0)
 
         def second_stage(i):
             npx = A_CHUNKS[i][2]
-            gr = grpool.tile([P, 4 * G * npx], BF16, name="gr", align_bytes=64)
-            tv = t_tiles[i][:].rearrange("p t (c i) -> p c t i", i=4)
-            nc.vector.tensor_tensor(
-                out=gr[:].rearrange("p (c i t) -> p c t i", i=4, t=4),
-                in0=tv[:, :, 0:4, :],
-                in1=tv[:, :, 2:6, :],
-                op=SUB,
-            )
+            gr = grpool.tile([P, 2, 4 * npx], BF16, name="gr", align_bytes=64)
+            tv = t_tiles[i][:].rearrange("p d u h (c i) -> p d c (u h) i", i=4)
+            gv = gr[:].rearrange("p v (c i t) -> p v c t i", i=4, t=4)
+            for v, op in ((0, ADD), (1, SUB)):
+                nc.vector.tensor_tensor(out=gv[:, v], in0=tv[:, 0], in1=tv[:, 1], op=op)
             gr_tiles[("a", i)] = gr
 
-        def split_rows(k, g):
-            xr = xrpool.tile([P, 2, 8, P], BF16, name="xr")
-            src = x_tiles[("c", k)][:, 2048 * g : 2048 * (g + 1)].rearrange("p (r h c) -> p h r c", h=2, c=64)
-            nc.scalar.copy(out=xr[:].rearrange("p h a (d c) -> p h (a d) c", d=2), in_=src)
-            xr_tiles[(k, g)] = xr
+        def split_rows(k):
+            xr = xrpool.tile([P, 2, 2, 8, P], BF16, name="xr")
+            src = x_tiles[("c", k)][:].rearrange("p u (r hh c) -> p hh (u r) c", hh=2, c=64)
+            nc.scalar.copy(out=xr[:].rearrange("p hh u a (d c) -> p hh (u a d) c", d=2), in_=src)
+            xr_tiles[k] = xr
 
         def turn(item):
-            k, g, q = item // 4, item // 2 % 2, item % 2
+            k, q = divmod(item, 4)
             if q == 0:
-                split_rows(k, g)
+                split_rows(k)
             tb = turnpool.tile([P, 8, P], BF16, name="tb")
             for b in range(8):
-                a, h = 4 * q + b // 2, b % 2
-                nc.tensor.transpose(tb[:, b, :], xr_tiles[(k, g)][:, h, a, :], identb[:])
+                a, hh, u = 2 * q + b // 4, b // 2 % 2, b % 2
+                nc.tensor.transpose(tb[:, b, :], xr_tiles[k][:, hh, u, a, :], identb[:])
             turn_tiles[item] = tb
 
         def take_turned(item):
-            xt = xtpool.tile([P, 8, P], BF16, name="xturned")
+            xt = xtpool.tile([P, 8, P], BF16, name="turned")
             nc.scalar.copy(out=xt[:], in_=turn_tiles[item][:])
             turned_tiles[item] = xt
 
         def make_bands(item):
-            bb = bandpool.tile([P, 8, P], BF16, name="bb")
+            bb = bandpool.tile([P, 2, 128, 2, 2], BF16, name="bb")
             for b in range(8):
-                nc.tensor.matmul(bb[:, b, :], lhsT=turned_tiles[item][:, b, :], rhs=haar[:], start=True, stop=True)
+                pixels, u = slice(32 * (b // 2), 32 * (b // 2 + 1)), b % 2
+                nc.tensor.matmul(
+                    bb[:, :, pixels, u, :],
+                    lhsT=turned_tiles[item][:, b, :],
+                    rhs=haar[:],
+                    start=True,
+                    stop=True,
+                )
             band_tiles[item] = bb
 
         def take_bands(item):
-            k, gq = divmod(item, 4)
-            if gq == 0:
-                gr_tiles[("c", k)] = grcpool.tile([P, 4 * G * 512], BF16, name="grc", align_bytes=64)
+            k, q = divmod(item, 4)
+            if q == 0:
+                gr_tiles[("c", k)] = grcpool.tile([P, 2, 4 * 512], BF16, name="grc", align_bytes=64)
             nc.scalar.copy(
-                out=gr_tiles[("c", k)][:, 1024 * gq : 1024 * (gq + 1)],
-                in_=band_tiles[item][:].rearrange("p b f -> p (b f)"),
+                out=gr_tiles[("c", k)][:, :, 512 * q : 512 * (q + 1)],
+                in_=band_tiles[item][:].rearrange("p v x u h -> p v (x u h)"),
             )
+
+        def run_slot(slot):
+            if slot < C_ITEMS:
+                turn(slot)
+            if 0 <= slot - 1 < C_ITEMS:
+                take_turned(slot - 1)
+                make_bands(slot - 1)
+            if slot >= 2:
+                take_bands(slot - 2)
 
         def quantise(job):
             npx = place(job)[2]
-            codes = qpool.tile([P, G * npx], U32, name="codes", align_bytes=64)
-            scales = qpool.tile([P, G * npx], U8, name="scales", align_bytes=64)
-            nc.vector.quantize_mx(out=codes[:].bitcast(FP8X4), scales=scales[:], in_=gr_tiles[job][:])
+            codes = qpool.tile([P, 2 * npx], U32, name="codes", align_bytes=64)
+            scales = qpool.tile([P, 2 * npx], U8, name="scales", align_bytes=64)
+            nc.vector.quantize_mx(
+                out=codes[:].bitcast(FP8X4), scales=scales[:], in_=gr_tiles[job][:].rearrange("p v f -> p (v f)")
+            )
             q_tiles[job] = (codes, scales)
 
-        def multiply(job):
+        def banks_of(job):
+            npx = place(job)[2]
+            return [(job, b) for b in range(MT * npx // BANK)]
+
+        def multiply(job, b):
             npx = place(job)[2]
             codes, scales = q_tiles[job]
             per_bank = BANK // npx
-            banks = []
-            for b in range(MT // per_bank):
-                acc = accpool.tile([P, per_bank, npx], F32, name="acc", tag="acc")
-                for s in range(per_bank):
-                    m = b * per_bank + s
-                    for g in range(G):
-                        wcols = slice(512 * g + P * m, 512 * g + P * (m + 1))
-                        xcols = slice(npx * g, npx * (g + 1))
-                        nc.tensor.matmul_mx(
-                            out=acc[:, s, :],
-                            lhsT=w_codes[:, wcols].bitcast(FP8X4),
-                            lhsT_scale=w_scales[:, wcols],
-                            rhs=codes[:, xcols].bitcast(FP8X4),
-                            rhs_scale=scales[:, xcols],
-                            start=(g == 0),
-                            stop=(g == G - 1),
-                        )
-                banks.append(acc)
-            acc_tiles[job] = banks
+            acc = accpool.tile([P, per_bank, npx], F32, name="acc", tag="acc")
+            for s in range(per_bank):
+                m = b * per_bank + s
+                for v in range(2):
+                    wcols = slice(512 * v + P * m, 512 * v + P * (m + 1))
+                    xcols = slice(npx * v, npx * (v + 1))
+                    nc.tensor.matmul_mx(
+                        out=acc[:, s, :],
+                        lhsT=w_codes[:, wcols].bitcast(FP8X4),
+                        lhsT_scale=w_scales[:, wcols],
+                        rhs=codes[:, xcols].bitcast(FP8X4),
+                        rhs_scale=scales[:, xcols],
+                        start=(v == 0),
+                        stop=(v == 1),
+                    )
+            filled.append((job, b, acc))
 
-        def evacuate(job):
+        def evacuate():
+            job, b, acc = filled.pop(0)
             n, p0, npx = place(job)
             per_bank = BANK // npx
-            if job[0] == "a" and job[1] >= NA - 3:
-                ot = xpool.tile([P, MT, npx], F32, name="xt")
-            else:
-                ot = opool.tile([P, MT, npx], F32, name="ot")
-            for b, acc in enumerate(acc_tiles[job]):
-                nc.scalar.activation(
-                    out=ot[:, b * per_bank : (b + 1) * per_bank, :], in_=acc[:], func=COPY, scale=0.5
-                )
-            dst = out[n].rearrange("(m p) i j -> p m (i j)", m=MT)
-            nc.scalar.dma_start(out=dst[:, :, p0 : p0 + npx], in_=ot[:])
+            if b == 0:
+                out_tiles[job] = opool.tile([P, MT, npx], F32, name="ot")
+            ot = out_tiles[job]
+            nc.scalar.activation(out=ot[:, b * per_bank : (b + 1) * per_bank, :], in_=acc[:], func=COPY, scale=0.5)
+            if b == MT // per_bank - 1:
+                dst = out[n].rearrange("(m p) i j -> p m (i j)", m=MT)
+                nc.scalar.dma_start(out=dst[:, :, p0 : p0 + npx], in_=ot[:])
 
-        w_sb = const.tile([P, MT * 1024], BF16, name="w_sb")
-        w_grouped = wgpool.tile([P, G * 512 * 4], BF16, name="w_grouped", align_bytes=64)
-        w_codes = const.tile([P, G * 512], U32, name="w_codes", align_bytes=64)
-        w_scales = const.tile([P, G * 512], U8, name="w_scales", align_bytes=64)
+        w_sb = const.tile([P, MT, 2, 512], BF16, name="w_sb")
+        w_grouped = const.tile([P, 2, 512 * 4], BF16, name="w_grouped", align_bytes=64)
+        w_codes = const.tile([P, 2 * 512], U32, name="w_codes", align_bytes=64)
+        w_scales = const.tile([P, 2 * 512], U8, name="w_scales", align_bytes=64)
 
-        def transpose_w():
-            w32 = w_sb[:].bitcast(F32)
-            wg32 = w_grouped[:].bitcast(F32)
-            for g in range(G):
-                for mp in range(MT // 2):
-                    wt = accpool.tile([P, 2, 2, P], F32, name="wt", tag="acc")
-                    for mm in range(2):
-                        for u in range(2):
-                            first = 512 * (2 * mp + mm) + 256 * g + u
-                            nc.tensor.transpose(wt[:, mm, 1 - u, :], w32[:, first : first + 255 : 2], ident32[:])
-                    nc.scalar.copy(
-                        out=wg32[:, 1024 * g + 512 * mp : 1024 * g + 512 * (mp + 1)].rearrange(
-                            "p (m o u) -> p m o u", m=2, u=2
-                        ),
-                        in_=wt[:].rearrange("p m u o -> p m o u"),
+        def load_w():
+            src = w_fusion.rearrange("(m p) (s u k) a b -> m u p s (k a b)", m=MT, s=4, u=2)
+            for m in range(MT):
+                for u in range(2):
+                    nc.sync.dma_start(
+                        out=w_sb[:, m, u, :].rearrange("p (s k) -> p s k", s=4), in_=src[m, u]
                     )
 
-        load(("a", 0))
-        load(("a", 1))
-        load(("a", 2))
-        nc.sync.dma_start(
-            out=w_sb[:].rearrange("p (m k) -> p m k", m=MT),
-            in_=w_fusion.rearrange("(m p) k a b -> p m (k a b)", m=MT),
-        )
-        load(("c", 0))
-        load(("a", 3))
+        def transpose_w():
+            for v in range(2):
+                for oh in range(2):
+                    wt = accpool.tile([P, 4, 256], BF16, name="wt", tag="acc")
+                    for t in range(4):
+                        u, h = divmod(t, 2)
+                        first = 2 * h + v
+                        for mm in range(2):
+                            nc.tensor.transpose(
+                                wt[:, t, P * mm : P * (mm + 1)],
+                                w_sb[:, 2 * oh + mm, u, first : first + 509 : 4],
+                                identb[:],
+                            )
+                    nc.scalar.copy(
+                        out=w_grouped[:, v, 1024 * oh : 1024 * (oh + 1)].rearrange("p (c i t) -> p c t i", i=4, t=4),
+                        in_=wt[:].rearrange("p t (c i) -> p c t i", i=4),
+                    )
 
-        ident32 = const.tile([P, P], F32, name="ident32")
-        make_identity(nc, ident32[:])
+        both = (nc.sync, nc.gpsimd)
+        load(("a", 0), (nc.sync, nc.sync))
+        load(("a", 1), (nc.sync, nc.sync))
+        load(("a", 2), both)
+        load(("c", 0), both)
+
         identb = const.tile([P, P], BF16, name="identb")
         make_identity(nc, identb[:])
         h2 = const.tile([P, 2, 32, 2], BF16, name="h2")
-        haar = const.tile([P, P], BF16, name="haar")
+        haar = const.tile([P, 2, 32, 2], BF16, name="haar")
         iv = identb[:].rearrange("p (d j e) -> p d j e", d=2, e=2)
-        nc.vector.tensor_tensor(out=h2[:, :, :, 0], in0=iv[:, :, :, 0], in1=iv[:, :, :, 1], op=ADD)
-        nc.vector.tensor_tensor(out=h2[:, :, :, 1], in0=iv[:, :, :, 0], in1=iv[:, :, :, 1], op=SUB)
-        hw = haar[:].rearrange("p (j h v) -> p j h v", h=2, v=2)
-        for h in range(2):
-            for v, op in ((0, ADD), (1, SUB)):
-                nc.vector.tensor_tensor(out=hw[:, :, 1 - h, v], in0=h2[:, 0, :, h], in1=h2[:, 1, :, h], op=op)
+        for h, op in ((0, ADD), (1, SUB)):
+            nc.vector.tensor_tensor(out=h2[:, :, :, h], in0=iv[:, :, :, 0], in1=iv[:, :, :, 1], op=op)
+        for v, op in ((0, ADD), (1, SUB)):
+            nc.vector.tensor_tensor(out=haar[:, v], in0=h2[:, 0], in1=h2[:, 1], op=op)
 
+        load_w()
+        load(("a", 3), both)
         first_stage(0)
-        negate(0)
-        load(("a", 4))
-        load(("c", 1))
+        load(("a", 4), both)
+        load(("c", 1), both)
 
         due = [[] for step in range(NA + 4)]
         slot = 0
@@ -246,35 +260,34 @@ def tile_haarwaveletlayer_t_kernel(tc, x, w_fusion, out):
             if i + 1 < NA:
                 first_stage(i + 1)
                 if i + 5 < NA:
-                    load(("a", i + 5))
+                    load(("a", i + 5), both)
             while loaded_c < N_C and loaded_c < slot // 4 + 3:
-                load(("c", loaded_c))
+                load(("c", loaded_c), both)
                 loaded_c += 1
+            if 1 <= i <= NA:
+                quantise(("a", i - 1))
+                due[max(i, 3)].append(("a", i - 1))
             if i < NA:
                 second_stage(i)
             if quantised_c < finished_c:
                 quantise(("c", quantised_c))
                 due[max(i + 1, 3)].append(("c", quantised_c))
                 quantised_c += 1
-            if i == 2:
+            if i == 1:
                 transpose_w()
-            for job in due[i]:
-                multiply(job)
-                evacuate(job)
-            if i + 1 < NA:
-                negate(i + 1)
-            if i < len(C_SLOTS):
-                for rep in range(C_SLOTS[i]):
-                    if slot < C_ITEMS:
-                        turn(slot)
-                    if 0 <= slot - 1 < C_ITEMS:
-                        take_turned(slot - 1)
-                        make_bands(slot - 1)
-                    if 0 <= slot - 2:
-                        take_bands(slot - 2)
-                    slot += 1
-            if 1 <= i <= NA:
-                quantise(("a", i - 1))
-                due[max(i + 1, 3)].append(("a", i - 1))
             if i == 2:
-                nc.vector.quantize_mx(out=w_codes[:].bitcast(FP8X4), scales=w_scales[:], in_=w_grouped[:])
+                nc.vector.quantize_mx(
+                    out=w_codes[:].bitcast(FP8X4), scales=w_scales[:], in_=w_grouped[:].rearrange("p v f -> p (v f)")
+                )
+            banks = [bank for job in due[i] for bank in banks_of(job)]
+            slots = C_SLOTS[i] if i < len(C_SLOTS) else 0
+            for rep in range(slots + 1):
+                for bank in banks[len(banks) * rep // (slots + 1) : len(banks) * (rep + 1) // (slots + 1)]:
+                    multiply(*bank)
+                    if len(filled) > EVAC_LAG:
+                        evacuate()
+                if rep < slots:
+                    run_slot(slot)
+                    slot += 1
+        while filled:
+            evacuate()

@@ -39,7 +39,7 @@ def tile_haarwaveletlayer_t_kernel(tc, x, w_fusion, out):
     nc = tc.nc
     with ExitStack() as ctx:
         const = ctx.enter_context(tc.tile_pool(name="const", bufs=1))
-        xpool = ctx.enter_context(tc.tile_pool(name="xpool", bufs=4))
+        xpool = ctx.enter_context(tc.tile_pool(name="xpool", bufs=5))
         xcpool = ctx.enter_context(tc.tile_pool(name="xcpool", bufs=3))
         xrpool = ctx.enter_context(tc.tile_pool(name="xrpool", bufs=2))
         xtpool = ctx.enter_context(tc.tile_pool(name="xtpool", bufs=3))
@@ -69,15 +69,13 @@ def tile_haarwaveletlayer_t_kernel(tc, x, w_fusion, out):
                 return A_CHUNKS[job[1]]
             return (C_IMAGE, C_FIRST + 512 * job[1], 512)
 
-        def load(job, queues):
+        def load(job):
             n, p0, npx = place(job)
             pool = xpool if job[0] == "a" else xcpool
             xt = pool.tile([P, 2, 4 * npx], BF16, name="xt")
-            src = x[n].rearrange("(s u r) h w -> s r u (h w)", s=4, u=2)
-            for s in range(4):
-                queues[s // 2].dma_start(
-                    out=xt[32 * s : 32 * (s + 1), :, :], in_=src[s, :, :, 4 * p0 : 4 * (p0 + npx)]
-                )
+            src = x[n].rearrange("(g u r) h w -> g r u (h w)", g=2, u=2)
+            for g, queue in ((0, nc.sync), (1, nc.scalar)):
+                queue.dma_start(out=xt[64 * g : 64 * (g + 1), :, :], in_=src[g, :, :, 4 * p0 : 4 * (p0 + npx)])
             x_tiles[job] = xt
 
         def first_stage(i):
@@ -204,12 +202,10 @@ def tile_haarwaveletlayer_t_kernel(tc, x, w_fusion, out):
         w_scales = const.tile([P, 2 * 512], U8, name="w_scales", align_bytes=64)
 
         def load_w():
-            src = w_fusion.rearrange("(m p) (s u k) a b -> m u p s (k a b)", m=MT, s=4, u=2)
-            for m in range(MT):
-                for u in range(2):
-                    nc.sync.dma_start(
-                        out=w_sb[:, m, u, :].rearrange("p (s k) -> p s k", s=4), in_=src[m, u]
-                    )
+            src = w_fusion.rearrange("(m p) (g u k) a b -> g u p m (k a b)", m=MT, g=2, u=2)
+            for u in range(2):
+                for g in range(2):
+                    nc.sync.dma_start(out=w_sb[:, :, u, 256 * g : 256 * (g + 1)], in_=src[g, u])
 
         def transpose_w():
             for v in range(2):
@@ -229,11 +225,9 @@ def tile_haarwaveletlayer_t_kernel(tc, x, w_fusion, out):
                         in_=wt[:].rearrange("p t (c i) -> p c t i", i=4),
                     )
 
-        both = (nc.sync, nc.gpsimd)
-        load(("a", 0), (nc.sync, nc.sync))
-        load(("a", 1), (nc.sync, nc.sync))
-        load(("a", 2), both)
-        load(("c", 0), both)
+        load(("a", 0))
+        load(("a", 1))
+        load(("a", 2))
 
         identb = const.tile([P, P], BF16, name="identb")
         make_identity(nc, identb[:])
@@ -246,10 +240,11 @@ def tile_haarwaveletlayer_t_kernel(tc, x, w_fusion, out):
             nc.vector.tensor_tensor(out=haar[:, v], in0=h2[:, 0], in1=h2[:, 1], op=op)
 
         load_w()
-        load(("a", 3), both)
+        load(("c", 0))
+        load(("a", 3))
         first_stage(0)
-        load(("a", 4), both)
-        load(("c", 1), both)
+        load(("a", 4))
+        load(("c", 1))
 
         due = [[] for step in range(NA + 4)]
         slot = 0
@@ -260,9 +255,9 @@ def tile_haarwaveletlayer_t_kernel(tc, x, w_fusion, out):
             if i + 1 < NA:
                 first_stage(i + 1)
                 if i + 5 < NA:
-                    load(("a", i + 5), both)
+                    load(("a", i + 5))
             while loaded_c < N_C and loaded_c < slot // 4 + 3:
-                load(("c", loaded_c), both)
+                load(("c", loaded_c))
                 loaded_c += 1
             if 1 <= i <= NA:
                 quantise(("a", i - 1))

@@ -18,17 +18,15 @@ P = 128
 MT = 4
 BANK = 512
 
-N_C = 6
-C_IMAGE = 1
-C_FIRST = 4096 - 512 * N_C
-C_SLOTS = (0, 2, 3, 3, 3, 3, 3, 3, 3, 3)
-C_ITEMS = 4 * N_C
-LAST_A = 512 * (7 - N_C)
+C_FIRST = 1024 - 128
+C_CHUNKS = [(1, C_FIRST, 128)] + [(1, 512 * r, 512) for r in range(2, 8)]
+C_ITEM_LIST = [(k, q) for k, chunk in enumerate(C_CHUNKS) for q in range(chunk[2] // 128)]
+C_ITEMS = len(C_ITEM_LIST)
+C_SLOTS = (0, 3, 3, 3, 3, 3, 3, 3, 3, 3)
 A_CHUNKS = (
     [(0, 0, 128), (0, 128, 128), (0, 256, 256)]
     + [(0, 512 * r, 512) for r in range(1, 8)]
-    + [(1, 512 * r, 512) for r in range(7 - N_C)]
-    + [(1, LAST_A, 256), (1, LAST_A + 256, 128), (1, LAST_A + 384, 128)]
+    + [(1, 0, 512), (1, 512, 256), (1, 768, 128)]
 )
 NA = len(A_CHUNKS)
 EVAC_LAG = 2
@@ -45,7 +43,7 @@ def tile_haarwaveletlayer_t_kernel(tc, x, w_fusion, out):
         xtpool = ctx.enter_context(tc.tile_pool(name="xtpool", bufs=3))
         tpool = ctx.enter_context(tc.tile_pool(name="tpool", bufs=2))
         grpool = ctx.enter_context(tc.tile_pool(name="grpool", bufs=2))
-        grcpool = ctx.enter_context(tc.tile_pool(name="grcpool", bufs=2))
+        grcpool = ctx.enter_context(tc.tile_pool(name="grcpool", bufs=3))
         qpool = ctx.enter_context(tc.tile_pool(name="qpool", bufs=4))
         opool = ctx.enter_context(tc.tile_pool(name="opool", bufs=4))
         accpool = ctx.enter_context(tc.psum_pool(name="accpool", bufs=4))
@@ -65,16 +63,14 @@ def tile_haarwaveletlayer_t_kernel(tc, x, w_fusion, out):
         filled = []
 
         def place(job):
-            if job[0] == "a":
-                return A_CHUNKS[job[1]]
-            return (C_IMAGE, C_FIRST + 512 * job[1], 512)
+            return (A_CHUNKS if job[0] == "a" else C_CHUNKS)[job[1]]
 
-        def load(job):
+        def load(job, queues=(nc.sync, nc.sync)):
             n, p0, npx = place(job)
             pool = xpool if job[0] == "a" else xcpool
             xt = pool.tile([P, 2, 4 * npx], BF16, name="xt")
             src = x[n].rearrange("(g u r) h w -> g r u (h w)", g=2, u=2)
-            for g, queue in ((0, nc.sync), (1, nc.scalar)):
+            for g, queue in enumerate(queues):
                 queue.dma_start(out=xt[64 * g : 64 * (g + 1), :, :], in_=src[g, :, :, 4 * p0 : 4 * (p0 + npx)])
             x_tiles[job] = xt
 
@@ -92,20 +88,20 @@ def tile_haarwaveletlayer_t_kernel(tc, x, w_fusion, out):
         def second_stage(i):
             npx = A_CHUNKS[i][2]
             gr = grpool.tile([P, 2, 4 * npx], BF16, name="gr", align_bytes=64)
-            tv = t_tiles[i][:].rearrange("p d u h (c i) -> p d c (u h) i", i=4)
-            gv = gr[:].rearrange("p v (c i t) -> p v c t i", i=4, t=4)
+            tv = t_tiles[i][:].rearrange("p d u h (c i) -> p d c (u h) i", i=2)
+            gv = gr[:].rearrange("p v (c i t) -> p v c t i", i=2, t=4)
             for v, op in ((0, ADD), (1, SUB)):
                 nc.vector.tensor_tensor(out=gv[:, v], in0=tv[:, 0], in1=tv[:, 1], op=op)
             gr_tiles[("a", i)] = gr
 
         def split_rows(k):
-            xr = xrpool.tile([P, 2, 2, 8, P], BF16, name="xr")
-            src = x_tiles[("c", k)][:].rearrange("p u (r hh c) -> p hh (u r) c", hh=2, c=64)
-            nc.scalar.copy(out=xr[:].rearrange("p hh u a (d c) -> p hh (u a d) c", d=2), in_=src)
+            xr = xrpool.tile([P, 2, 2, C_CHUNKS[k][2] // 64, P], BF16, name="xr")
+            src = x_tiles[("c", k)][:].bitcast(F32).rearrange("p u (r hh c) -> p hh (u r) c", hh=2, c=32)
+            nc.scalar.copy(out=xr[:].bitcast(F32).rearrange("p hh u a (d c) -> p hh (u a d) c", d=2), in_=src)
             xr_tiles[k] = xr
 
         def turn(item):
-            k, q = divmod(item, 4)
+            k, q = C_ITEM_LIST[item]
             if q == 0:
                 split_rows(k)
             tb = turnpool.tile([P, 8, P], BF16, name="tb")
@@ -116,7 +112,7 @@ def tile_haarwaveletlayer_t_kernel(tc, x, w_fusion, out):
 
         def take_turned(item):
             xt = xtpool.tile([P, 8, P], BF16, name="turned")
-            nc.scalar.copy(out=xt[:], in_=turn_tiles[item][:])
+            nc.scalar.copy(out=xt[:].bitcast(F32), in_=turn_tiles[item][:].bitcast(F32))
             turned_tiles[item] = xt
 
         def make_bands(item):
@@ -133,12 +129,12 @@ def tile_haarwaveletlayer_t_kernel(tc, x, w_fusion, out):
             band_tiles[item] = bb
 
         def take_bands(item):
-            k, q = divmod(item, 4)
+            k, q = C_ITEM_LIST[item]
             if q == 0:
-                gr_tiles[("c", k)] = grcpool.tile([P, 2, 4 * 512], BF16, name="grc", align_bytes=64)
+                gr_tiles[("c", k)] = grcpool.tile([P, 2, 4 * C_CHUNKS[k][2]], BF16, name="grc", align_bytes=64)
             nc.scalar.copy(
-                out=gr_tiles[("c", k)][:, :, 512 * q : 512 * (q + 1)],
-                in_=band_tiles[item][:].rearrange("p v x u h -> p v (x u h)"),
+                out=gr_tiles[("c", k)][:, :, 512 * q : 512 * (q + 1)].bitcast(F32),
+                in_=band_tiles[item][:].rearrange("p v x u h -> p v (x u h)").bitcast(F32),
             )
 
         def run_slot(slot):
@@ -191,7 +187,7 @@ def tile_haarwaveletlayer_t_kernel(tc, x, w_fusion, out):
             if b == 0:
                 out_tiles[job] = opool.tile([P, MT, npx], F32, name="ot")
             ot = out_tiles[job]
-            nc.scalar.activation(out=ot[:, b * per_bank : (b + 1) * per_bank, :], in_=acc[:], func=COPY, scale=0.5)
+            nc.scalar.copy(out=ot[:, b * per_bank : (b + 1) * per_bank, :], in_=acc[:])
             if b == MT // per_bank - 1:
                 dst = out[n].rearrange("(m p) i j -> p m (i j)", m=MT)
                 nc.scalar.dma_start(out=dst[:, :, p0 : p0 + npx], in_=ot[:])
@@ -220,14 +216,17 @@ def tile_haarwaveletlayer_t_kernel(tc, x, w_fusion, out):
                                 w_sb[:, 2 * oh + mm, u, first : first + 509 : 4],
                                 identb[:],
                             )
-                    nc.scalar.copy(
+                    nc.scalar.activation(
                         out=w_grouped[:, v, 1024 * oh : 1024 * (oh + 1)].rearrange("p (c i t) -> p c t i", i=4, t=4),
                         in_=wt[:].rearrange("p t (c i) -> p c t i", i=4),
+                        func=COPY,
+                        scale=0.5,
                     )
 
-        load(("a", 0))
-        load(("a", 1))
-        load(("a", 2))
+        both = (nc.sync, nc.scalar)
+        load(("a", 0), both)
+        load(("a", 1), both)
+        load(("a", 2), both)
 
         identb = const.tile([P, P], BF16, name="identb")
         make_identity(nc, identb[:])
@@ -240,7 +239,7 @@ def tile_haarwaveletlayer_t_kernel(tc, x, w_fusion, out):
             nc.vector.tensor_tensor(out=haar[:, v], in0=h2[:, 0], in1=h2[:, 1], op=op)
 
         load_w()
-        load(("c", 0))
+        load(("c", 0), both)
         load(("a", 3))
         first_stage(0)
         load(("a", 4))
@@ -250,13 +249,15 @@ def tile_haarwaveletlayer_t_kernel(tc, x, w_fusion, out):
         slot = 0
         loaded_c = 2
         quantised_c = 0
+        done = []
         for i in range(NA + 3):
-            finished_c = max(slot - 2, 0) // 4
+            ready, done = done, C_ITEM_LIST[: max(slot - 2, 0)]
+            started_c = C_ITEM_LIST[min(slot, C_ITEMS - 1)][0]
             if i + 1 < NA:
                 first_stage(i + 1)
                 if i + 5 < NA:
                     load(("a", i + 5))
-            while loaded_c < N_C and loaded_c < slot // 4 + 3:
+            while loaded_c < len(C_CHUNKS) and loaded_c < started_c + 3:
                 load(("c", loaded_c))
                 loaded_c += 1
             if 1 <= i <= NA:
@@ -264,7 +265,7 @@ def tile_haarwaveletlayer_t_kernel(tc, x, w_fusion, out):
                 due[max(i, 3)].append(("a", i - 1))
             if i < NA:
                 second_stage(i)
-            if quantised_c < finished_c:
+            while quantised_c < len(C_CHUNKS) and (quantised_c, C_CHUNKS[quantised_c][2] // 128 - 1) in ready:
                 quantise(("c", quantised_c))
                 due[max(i + 1, 3)].append(("c", quantised_c))
                 quantised_c += 1

@@ -22,10 +22,10 @@ C_FIRST = 1024 - 128
 C_CHUNKS = [(1, C_FIRST, 128)] + [(1, 512 * r, 512) for r in range(2, 8)]
 C_ITEM_LIST = [(k, q) for k, chunk in enumerate(C_CHUNKS) for q in range(chunk[2] // 128)]
 C_ITEMS = len(C_ITEM_LIST)
-C_SLOTS = (0, 3, 3, 3, 3, 3, 3, 3, 3, 3)
+C_SLOTS = (0, 0, 1, 1, 3, 4, 4, 4, 4, 4, 2)
 A_CHUNKS = (
-    [(0, 0, 128), (0, 128, 128), (0, 256, 256)]
-    + [(0, 512 * r, 512) for r in range(1, 8)]
+    [(0, 0, 128), (0, 128, 128), (0, 256, 256), (0, 512, 256), (0, 768, 256)]
+    + [(0, 512 * r, 512) for r in range(2, 8)]
     + [(1, 0, 512), (1, 512, 256), (1, 768, 128)]
 )
 NA = len(A_CHUNKS)
@@ -65,13 +65,18 @@ def tile_haarwaveletlayer_t_kernel(tc, x, w_fusion, out):
         def place(job):
             return (A_CHUNKS if job[0] == "a" else C_CHUNKS)[job[1]]
 
-        def load(job, queues=(nc.sync, nc.sync)):
+        def load(job):
             n, p0, npx = place(job)
-            pool = xpool if job[0] == "a" else xcpool
-            xt = pool.tile([P, 2, 4 * npx], BF16, name="xt")
-            src = x[n].rearrange("(g u r) h w -> g r u (h w)", g=2, u=2)
-            for g, queue in enumerate(queues):
-                queue.dma_start(out=xt[64 * g : 64 * (g + 1), :, :], in_=src[g, :, :, 4 * p0 : 4 * (p0 + npx)])
+            pixels = slice(4 * p0, 4 * (p0 + npx))
+            if job[0] == "a":
+                xt = xpool.tile([P, 2, 4 * npx], BF16, name="xt")
+                src = x[n].rearrange("c h w -> c (h w)")[:, pixels]
+                nc.sync.dma_start(out=xt[:, 0, :], in_=src[64:192])
+                nc.sync.dma_start(out=xt[0:64, 1, :], in_=src[0:64])
+                nc.sync.dma_start(out=xt[64:128, 1, :], in_=src[192:256])
+            else:
+                xt = xcpool.tile([P, 2, 4 * npx], BF16, name="xc")
+                nc.sync.dma_start(out=xt[:], in_=x[n].rearrange("(g p) h w -> p g (h w)", g=2)[:, :, pixels])
             x_tiles[job] = xt
 
         def first_stage(i):
@@ -96,8 +101,8 @@ def tile_haarwaveletlayer_t_kernel(tc, x, w_fusion, out):
 
         def split_rows(k):
             xr = xrpool.tile([P, 2, 2, C_CHUNKS[k][2] // 64, P], BF16, name="xr")
-            src = x_tiles[("c", k)][:].bitcast(F32).rearrange("p u (r hh c) -> p hh (u r) c", hh=2, c=32)
-            nc.scalar.copy(out=xr[:].bitcast(F32).rearrange("p hh u a (d c) -> p hh (u a d) c", d=2), in_=src)
+            src = x_tiles[("c", k)][:].bitcast(F32).rearrange("p g (r hh c) -> p hh (g r) c", hh=2, c=32)
+            nc.scalar.copy(out=xr[:].bitcast(F32).rearrange("p hh g a (d c) -> p hh (g a d) c", d=2), in_=src)
             xr_tiles[k] = xr
 
         def turn(item):
@@ -106,8 +111,8 @@ def tile_haarwaveletlayer_t_kernel(tc, x, w_fusion, out):
                 split_rows(k)
             tb = turnpool.tile([P, 8, P], BF16, name="tb")
             for b in range(8):
-                a, hh, u = 2 * q + b // 4, b // 2 % 2, b % 2
-                nc.tensor.transpose(tb[:, b, :], xr_tiles[k][:, hh, u, a, :], identb[:])
+                a, hh, g = 2 * q + b // 4, b // 2 % 2, b % 2
+                nc.tensor.transpose(tb[:, b, :], xr_tiles[k][:, hh, g, a, :], identb[:])
             turn_tiles[item] = tb
 
         def take_turned(item):
@@ -116,11 +121,10 @@ def tile_haarwaveletlayer_t_kernel(tc, x, w_fusion, out):
             turned_tiles[item] = xt
 
         def make_bands(item):
-            bb = bandpool.tile([P, 2, 128, 2, 2], BF16, name="bb")
+            bb = bandpool.tile([P, 2, 512], BF16, name="bb")
             for b in range(8):
-                pixels, u = slice(32 * (b // 2), 32 * (b // 2 + 1)), b % 2
                 nc.tensor.matmul(
-                    bb[:, :, pixels, u, :],
+                    bb[:, b % 2, P * (b // 2) : P * (b // 2 + 1)],
                     lhsT=turned_tiles[item][:, b, :],
                     rhs=haar[:],
                     start=True,
@@ -134,7 +138,7 @@ def tile_haarwaveletlayer_t_kernel(tc, x, w_fusion, out):
                 gr_tiles[("c", k)] = grcpool.tile([P, 2, 4 * C_CHUNKS[k][2]], BF16, name="grc", align_bytes=64)
             nc.scalar.copy(
                 out=gr_tiles[("c", k)][:, :, 512 * q : 512 * (q + 1)].bitcast(F32),
-                in_=band_tiles[item][:].rearrange("p v x u h -> p v (x u h)").bitcast(F32),
+                in_=band_tiles[item][:].bitcast(F32),
             )
 
         def run_slot(slot):
@@ -162,48 +166,63 @@ def tile_haarwaveletlayer_t_kernel(tc, x, w_fusion, out):
         def multiply(job, b):
             npx = place(job)[2]
             codes, scales = q_tiles[job]
+            w_codes, w_scales = w_quantised[job[0]]
             per_bank = BANK // npx
             acc = accpool.tile([P, per_bank, npx], F32, name="acc", tag="acc")
             for s in range(per_bank):
                 m = b * per_bank + s
-                for v in range(2):
-                    wcols = slice(512 * v + P * m, 512 * v + P * (m + 1))
-                    xcols = slice(npx * v, npx * (v + 1))
+                for s_k in range(2):
+                    wcols = slice(512 * s_k + P * m, 512 * s_k + P * (m + 1))
+                    xcols = slice(npx * s_k, npx * (s_k + 1))
                     nc.tensor.matmul_mx(
                         out=acc[:, s, :],
                         lhsT=w_codes[:, wcols].bitcast(FP8X4),
                         lhsT_scale=w_scales[:, wcols],
                         rhs=codes[:, xcols].bitcast(FP8X4),
                         rhs_scale=scales[:, xcols],
-                        start=(v == 0),
-                        stop=(v == 1),
+                        start=(s_k == 0),
+                        stop=(s_k == 1),
                     )
             filled.append((job, b, acc))
 
-        def evacuate():
+        def evacuate(copy=nc.scalar.copy):
             job, b, acc = filled.pop(0)
             n, p0, npx = place(job)
             per_bank = BANK // npx
             if b == 0:
-                out_tiles[job] = opool.tile([P, MT, npx], F32, name="ot")
+                out_tiles[job] = opool.tile([P, MT, npx], F32, name="ot", align_bytes=64)
             ot = out_tiles[job]
-            nc.scalar.copy(out=ot[:, b * per_bank : (b + 1) * per_bank, :], in_=acc[:])
+            copy(out=ot[:, b * per_bank : (b + 1) * per_bank, :], in_=acc[:])
             if b == MT // per_bank - 1:
                 dst = out[n].rearrange("(m p) i j -> p m (i j)", m=MT)
                 nc.scalar.dma_start(out=dst[:, :, p0 : p0 + npx], in_=ot[:])
 
-        w_sb = const.tile([P, MT, 2, 512], BF16, name="w_sb")
-        w_grouped = const.tile([P, 2, 512 * 4], BF16, name="w_grouped", align_bytes=64)
-        w_codes = const.tile([P, 2 * 512], U32, name="w_codes", align_bytes=64)
-        w_scales = const.tile([P, 2 * 512], U8, name="w_scales", align_bytes=64)
+        w_sb = const.tile([P, MT, 1024], BF16, name="w_sb")
+        w_outer = const.tile([P, MT, 512], BF16, name="w_outer")
+        w_grouped = {}
+        w_quantised = {
+            "a": (
+                const.tile([P, 2 * 512], U32, name="w_codes_a", align_bytes=64),
+                const.tile([P, 2 * 512], U8, name="w_scales_a", align_bytes=64),
+            ),
+            "c": (
+                const.tile([P, 2 * 512], U32, name="w_codes_c", align_bytes=64),
+                const.tile([P, 2 * 512], U8, name="w_scales_c", align_bytes=64),
+            ),
+        }
 
         def load_w():
-            src = w_fusion.rearrange("(m p) (g u k) a b -> g u p m (k a b)", m=MT, g=2, u=2)
-            for u in range(2):
-                for g in range(2):
-                    nc.sync.dma_start(out=w_sb[:, :, u, 256 * g : 256 * (g + 1)], in_=src[g, u])
+            src = w_fusion.rearrange("(m p) k a b -> p m (k a b)", m=MT)
+            nc.sync.dma_start(out=w_sb[:], in_=src)
 
-        def transpose_w():
+        def copy_w_outer():
+            quarters = w_sb[:].bitcast(F32).rearrange("p m (q k) -> p m q k", q=4)
+            nc.scalar.copy(
+                out=w_outer[:].bitcast(F32).rearrange("p m (q k) -> p m q k", q=2), in_=quarters[:, :, 0:4:3, :]
+            )
+
+        def transpose_w_a():
+            wg = opool.tile([P, 2, 512 * 4], BF16, name="ot", align_bytes=64)
             for v in range(2):
                 for oh in range(2):
                     wt = accpool.tile([P, 4, 256], BF16, name="wt", tag="acc")
@@ -211,47 +230,78 @@ def tile_haarwaveletlayer_t_kernel(tc, x, w_fusion, out):
                         u, h = divmod(t, 2)
                         first = 2 * h + v
                         for mm in range(2):
+                            m = 2 * oh + mm
+                            w_u = w_outer[:, m, :] if u else w_sb[:, m, 256:768]
                             nc.tensor.transpose(
-                                wt[:, t, P * mm : P * (mm + 1)],
-                                w_sb[:, 2 * oh + mm, u, first : first + 509 : 4],
-                                identb[:],
+                                wt[:, t, P * mm : P * (mm + 1)], w_u[:, first : first + 509 : 4], identb[:]
                             )
                     nc.scalar.activation(
-                        out=w_grouped[:, v, 1024 * oh : 1024 * (oh + 1)].rearrange("p (c i t) -> p c t i", i=4, t=4),
+                        out=wg[:, v, 1024 * oh : 1024 * (oh + 1)].rearrange("p (c i t) -> p c t i", i=4, t=4),
                         in_=wt[:].rearrange("p t (c i) -> p c t i", i=4),
                         func=COPY,
                         scale=0.5,
                     )
+            w_grouped["a"] = wg
 
-        both = (nc.sync, nc.scalar)
-        load(("a", 0), both)
-        load(("a", 1), both)
-        load(("a", 2), both)
+        def transpose_w_c():
+            wg = opool.tile([P, 2, 512 * 4], BF16, name="ot", align_bytes=64)
+            w32 = w_sb[:].bitcast(F32)
+            for g in range(2):
+                for oh in range(2):
+                    wt = accpool.tile([P, 2, 2, P], F32, name="wt32", tag="acc")
+                    for mm in range(2):
+                        for b in range(2):
+                            first = 256 * g + b
+                            nc.tensor.transpose(
+                                wt[:, mm, b, :], w32[:, 2 * oh + mm, first : first + 255 : 2], ident32[:]
+                            )
+                    nc.scalar.copy(
+                        out=wg[:, g, 1024 * oh : 1024 * (oh + 1)].bitcast(F32).rearrange("p (m o b) -> p m o b", m=2, b=2),
+                        in_=wt[:].rearrange("p m b o -> p m o b"),
+                    )
+            w_grouped["c"] = wg
+
+        def quantise_w(kind):
+            codes, scales = w_quantised[kind]
+            nc.vector.quantize_mx(
+                out=codes[:].bitcast(FP8X4), scales=scales[:], in_=w_grouped[kind][:].rearrange("p v f -> p (v f)")
+            )
+
+        load(("a", 0))
+        load(("a", 1))
+        load(("a", 2))
+        load(("c", 0))
+        load_w()
+        load(("a", 3))
+        load(("c", 1))
 
         identb = const.tile([P, P], BF16, name="identb")
         make_identity(nc, identb[:])
+        ident32 = const.tile([P, P], F32, name="ident32")
+        make_identity(nc, ident32[:])
+        halves = const.tile([P, P], BF16, name="halves")
         h2 = const.tile([P, 2, 32, 2], BF16, name="h2")
-        haar = const.tile([P, 2, 32, 2], BF16, name="haar")
-        iv = identb[:].rearrange("p (d j e) -> p d j e", d=2, e=2)
+        haar = const.tile([P, P], BF16, name="haar")
+        nc.vector.tensor_scalar_mul(out=halves[:], in0=identb[:], scalar1=0.5)
+        iv = halves[:].rearrange("p (d j e) -> p d j e", d=2, e=2)
         for h, op in ((0, ADD), (1, SUB)):
             nc.vector.tensor_tensor(out=h2[:, :, :, h], in0=iv[:, :, :, 0], in1=iv[:, :, :, 1], op=op)
+        hv = haar[:].rearrange("p (j h v) -> p v j h", h=2, v=2)
         for v, op in ((0, ADD), (1, SUB)):
-            nc.vector.tensor_tensor(out=haar[:, v], in0=h2[:, 0], in1=h2[:, 1], op=op)
+            nc.vector.tensor_tensor(out=hv[:, v], in0=h2[:, 0], in1=h2[:, 1], op=op)
 
-        load_w()
-        load(("c", 0), both)
-        load(("a", 3))
         first_stage(0)
         load(("a", 4))
-        load(("c", 1))
+
+        def evacuate_next(step):
+            evacuate(nc.vector.tensor_copy if step >= NA and filled[0][1] % 2 else nc.scalar.copy)
 
         due = [[] for step in range(NA + 4)]
         slot = 0
         loaded_c = 2
         quantised_c = 0
-        done = []
         for i in range(NA + 3):
-            ready, done = done, C_ITEM_LIST[: max(slot - 2, 0)]
+            done = C_ITEM_LIST[: max(slot - 2, 0)]
             started_c = C_ITEM_LIST[min(slot, C_ITEMS - 1)][0]
             if i + 1 < NA:
                 first_stage(i + 1)
@@ -265,25 +315,27 @@ def tile_haarwaveletlayer_t_kernel(tc, x, w_fusion, out):
                 due[max(i, 3)].append(("a", i - 1))
             if i < NA:
                 second_stage(i)
-            while quantised_c < len(C_CHUNKS) and (quantised_c, C_CHUNKS[quantised_c][2] // 128 - 1) in ready:
+            while quantised_c < len(C_CHUNKS) and (quantised_c, C_CHUNKS[quantised_c][2] // 128 - 1) in done:
                 quantise(("c", quantised_c))
-                due[max(i + 1, 3)].append(("c", quantised_c))
+                due[max(i + 1, 4)].append(("c", quantised_c))
                 quantised_c += 1
             if i == 1:
-                transpose_w()
+                copy_w_outer()
+                transpose_w_a()
             if i == 2:
-                nc.vector.quantize_mx(
-                    out=w_codes[:].bitcast(FP8X4), scales=w_scales[:], in_=w_grouped[:].rearrange("p v f -> p (v f)")
-                )
+                quantise_w("a")
+                transpose_w_c()
+            if i == 3:
+                quantise_w("c")
             banks = [bank for job in due[i] for bank in banks_of(job)]
             slots = C_SLOTS[i] if i < len(C_SLOTS) else 0
             for rep in range(slots + 1):
                 for bank in banks[len(banks) * rep // (slots + 1) : len(banks) * (rep + 1) // (slots + 1)]:
                     multiply(*bank)
                     if len(filled) > EVAC_LAG:
-                        evacuate()
+                        evacuate_next(i)
                 if rep < slots:
                     run_slot(slot)
                     slot += 1
         while filled:
-            evacuate()
+            evacuate_next(NA + 3)

@@ -22,7 +22,7 @@ C_FIRST = 1024 - 128
 C_CHUNKS = [(1, C_FIRST, 128)] + [(1, 512 * r, 512) for r in range(2, 8)]
 C_ITEM_LIST = [(k, q) for k, chunk in enumerate(C_CHUNKS) for q in range(chunk[2] // 128)]
 C_ITEMS = len(C_ITEM_LIST)
-C_SLOTS = (0, 0, 1, 1, 3, 4, 4, 4, 4, 4, 2)
+C_SLOTS = (0, 0, 1, 3, 3, 4, 4, 4, 3, 3, 2)
 A_CHUNKS = (
     [(0, 0, 128), (0, 128, 128), (0, 256, 256), (0, 512, 256), (0, 768, 256)]
     + [(0, 512 * r, 512) for r in range(2, 8)]
@@ -93,8 +93,8 @@ def tile_haarwaveletlayer_t_kernel(tc, x, w_fusion, out):
         def second_stage(i):
             npx = A_CHUNKS[i][2]
             gr = grpool.tile([P, 2, 4 * npx], BF16, name="gr", align_bytes=64)
-            tv = t_tiles[i][:].rearrange("p d u h (c i) -> p d c (u h) i", i=2)
-            gv = gr[:].rearrange("p v (c i t) -> p v c t i", i=2, t=4)
+            tv = t_tiles[i][:].rearrange("p d u h (c i) -> p d c (u h) i", i=4)
+            gv = gr[:].rearrange("p v (c i t) -> p v c t i", i=4, t=4)
             for v, op in ((0, ADD), (1, SUB)):
                 nc.vector.tensor_tensor(out=gv[:, v], in0=tv[:, 0], in1=tv[:, 1], op=op)
             gr_tiles[("a", i)] = gr
@@ -116,20 +116,24 @@ def tile_haarwaveletlayer_t_kernel(tc, x, w_fusion, out):
             turn_tiles[item] = tb
 
         def take_turned(item):
-            xt = xtpool.tile([P, 8, P], BF16, name="turned")
-            nc.scalar.copy(out=xt[:].bitcast(F32), in_=turn_tiles[item][:].bitcast(F32))
+            xt = xtpool.tile([P, 4, 256], BF16, name="turned")
+            src = turn_tiles[item][:].rearrange("p b c -> p (b c)").bitcast(F32).rearrange("p (b q c) -> p b q c", q=4, c=32)
+            dst = xt[:].bitcast(F32).rearrange("p b (q c) -> p b q c", c=32)
+            nc.scalar.copy(out=dst[:, :, 0:2, :], in_=src[:, :, 0:4:3, :])
+            nc.scalar.copy(out=dst[:, :, 2:4, :], in_=src[:, :, 1:3, :])
             turned_tiles[item] = xt
 
         def make_bands(item):
-            bb = bandpool.tile([P, 2, 512], BF16, name="bb")
-            for b in range(8):
-                nc.tensor.matmul(
-                    bb[:, b % 2, P * (b // 2) : P * (b // 2 + 1)],
-                    lhsT=turned_tiles[item][:, b, :],
-                    rhs=haar[:],
-                    start=True,
-                    stop=True,
-                )
+            bb = bandpool.tile([P, 2, 128, 2, 2], BF16, name="bb")
+            for b in range(4):
+                for u in range(2):
+                    nc.tensor.matmul(
+                        bb[:, :, 32 * b : 32 * (b + 1), u, :],
+                        lhsT=turned_tiles[item][:, b, P * (1 - u) : P * (2 - u)],
+                        rhs=haar[:],
+                        start=True,
+                        stop=True,
+                    )
             band_tiles[item] = bb
 
         def take_bands(item):
@@ -138,7 +142,7 @@ def tile_haarwaveletlayer_t_kernel(tc, x, w_fusion, out):
                 gr_tiles[("c", k)] = grcpool.tile([P, 2, 4 * C_CHUNKS[k][2]], BF16, name="grc", align_bytes=64)
             nc.scalar.copy(
                 out=gr_tiles[("c", k)][:, :, 512 * q : 512 * (q + 1)].bitcast(F32),
-                in_=band_tiles[item][:].bitcast(F32),
+                in_=band_tiles[item][:].rearrange("p v x u h -> p v (x u h)").bitcast(F32),
             )
 
         def run_slot(slot):
@@ -166,7 +170,6 @@ def tile_haarwaveletlayer_t_kernel(tc, x, w_fusion, out):
         def multiply(job, b):
             npx = place(job)[2]
             codes, scales = q_tiles[job]
-            w_codes, w_scales = w_quantised[job[0]]
             per_bank = BANK // npx
             acc = accpool.tile([P, per_bank, npx], F32, name="acc", tag="acc")
             for s in range(per_bank):
@@ -199,17 +202,8 @@ def tile_haarwaveletlayer_t_kernel(tc, x, w_fusion, out):
 
         w_sb = const.tile([P, MT, 1024], BF16, name="w_sb")
         w_outer = const.tile([P, MT, 512], BF16, name="w_outer")
-        w_grouped = {}
-        w_quantised = {
-            "a": (
-                const.tile([P, 2 * 512], U32, name="w_codes_a", align_bytes=64),
-                const.tile([P, 2 * 512], U8, name="w_scales_a", align_bytes=64),
-            ),
-            "c": (
-                const.tile([P, 2 * 512], U32, name="w_codes_c", align_bytes=64),
-                const.tile([P, 2 * 512], U8, name="w_scales_c", align_bytes=64),
-            ),
-        }
+        w_codes = const.tile([P, 2 * 512], U32, name="w_codes", align_bytes=64)
+        w_scales = const.tile([P, 2 * 512], U8, name="w_scales", align_bytes=64)
 
         def load_w():
             src = w_fusion.rearrange("(m p) k a b -> p m (k a b)", m=MT)
@@ -221,7 +215,7 @@ def tile_haarwaveletlayer_t_kernel(tc, x, w_fusion, out):
                 out=w_outer[:].bitcast(F32).rearrange("p m (q k) -> p m q k", q=2), in_=quarters[:, :, 0:4:3, :]
             )
 
-        def transpose_w_a():
+        def transpose_w():
             wg = opool.tile([P, 2, 512 * 4], BF16, name="ot", align_bytes=64)
             for v in range(2):
                 for oh in range(2):
@@ -241,31 +235,7 @@ def tile_haarwaveletlayer_t_kernel(tc, x, w_fusion, out):
                         func=COPY,
                         scale=0.5,
                     )
-            w_grouped["a"] = wg
-
-        def transpose_w_c():
-            wg = opool.tile([P, 2, 512 * 4], BF16, name="ot", align_bytes=64)
-            w32 = w_sb[:].bitcast(F32)
-            for g in range(2):
-                for oh in range(2):
-                    wt = accpool.tile([P, 2, 2, P], F32, name="wt32", tag="acc")
-                    for mm in range(2):
-                        for b in range(2):
-                            first = 256 * g + b
-                            nc.tensor.transpose(
-                                wt[:, mm, b, :], w32[:, 2 * oh + mm, first : first + 255 : 2], ident32[:]
-                            )
-                    nc.scalar.copy(
-                        out=wg[:, g, 1024 * oh : 1024 * (oh + 1)].bitcast(F32).rearrange("p (m o b) -> p m o b", m=2, b=2),
-                        in_=wt[:].rearrange("p m b o -> p m o b"),
-                    )
-            w_grouped["c"] = wg
-
-        def quantise_w(kind):
-            codes, scales = w_quantised[kind]
-            nc.vector.quantize_mx(
-                out=codes[:].bitcast(FP8X4), scales=scales[:], in_=w_grouped[kind][:].rearrange("p v f -> p (v f)")
-            )
+            return wg
 
         load(("a", 0))
         load(("a", 1))
@@ -277,18 +247,13 @@ def tile_haarwaveletlayer_t_kernel(tc, x, w_fusion, out):
 
         identb = const.tile([P, P], BF16, name="identb")
         make_identity(nc, identb[:])
-        ident32 = const.tile([P, P], F32, name="ident32")
-        make_identity(nc, ident32[:])
-        halves = const.tile([P, P], BF16, name="halves")
         h2 = const.tile([P, 2, 32, 2], BF16, name="h2")
-        haar = const.tile([P, P], BF16, name="haar")
-        nc.vector.tensor_scalar_mul(out=halves[:], in0=identb[:], scalar1=0.5)
-        iv = halves[:].rearrange("p (d j e) -> p d j e", d=2, e=2)
+        haar = const.tile([P, 2, 32, 2], BF16, name="haar")
+        iv = identb[:].rearrange("p (d j e) -> p d j e", d=2, e=2)
         for h, op in ((0, ADD), (1, SUB)):
             nc.vector.tensor_tensor(out=h2[:, :, :, h], in0=iv[:, :, :, 0], in1=iv[:, :, :, 1], op=op)
-        hv = haar[:].rearrange("p (j h v) -> p v j h", h=2, v=2)
         for v, op in ((0, ADD), (1, SUB)):
-            nc.vector.tensor_tensor(out=hv[:, v], in0=h2[:, 0], in1=h2[:, 1], op=op)
+            nc.vector.tensor_tensor(out=haar[:, v], in0=h2[:, 0], in1=h2[:, 1], op=op)
 
         first_stage(0)
         load(("a", 4))
@@ -317,16 +282,15 @@ def tile_haarwaveletlayer_t_kernel(tc, x, w_fusion, out):
                 second_stage(i)
             while quantised_c < len(C_CHUNKS) and (quantised_c, C_CHUNKS[quantised_c][2] // 128 - 1) in done:
                 quantise(("c", quantised_c))
-                due[max(i + 1, 4)].append(("c", quantised_c))
+                due[max(i + 1, 3)].append(("c", quantised_c))
                 quantised_c += 1
             if i == 1:
                 copy_w_outer()
-                transpose_w_a()
+                w_grouped = transpose_w()
             if i == 2:
-                quantise_w("a")
-                transpose_w_c()
-            if i == 3:
-                quantise_w("c")
+                nc.vector.quantize_mx(
+                    out=w_codes[:].bitcast(FP8X4), scales=w_scales[:], in_=w_grouped[:].rearrange("p v f -> p (v f)")
+                )
             banks = [bank for job in due[i] for bank in banks_of(job)]
             slots = C_SLOTS[i] if i < len(C_SLOTS) else 0
             for rep in range(slots + 1):

from contextlib import ExitStack

import concourse.mybir as mybir
from concourse.masks import make_identity

FLOPS = 2 * 2 * 4096 * 1024 * 512

F32 = mybir.dt.float32
BF16 = mybir.dt.bfloat16
U32 = mybir.dt.uint32
U8 = mybir.dt.uint8
FP8X4 = mybir.dt.float8_e4m3fn_x4
ADD = mybir.AluOpType.add
SUB = mybir.AluOpType.subtract
COPY = mybir.ActivationFunctionType.Copy

P = 128
MT = 4
BANK = 512

C_FIRST = 1024 - 128
C_CHUNKS = [(1, C_FIRST, 128)] + [(1, 512 * r, 512) for r in range(2, 8)]
C_ITEM_LIST = [(k, q) for k, chunk in enumerate(C_CHUNKS) for q in range(chunk[2] // 128)]
C_ITEMS = len(C_ITEM_LIST)
C_SLOTS = (0, 0, 1, 3, 3, 4, 4, 4, 3, 3, 2)
A_CHUNKS = (
    [(0, 0, 128), (0, 128, 128), (0, 256, 256), (0, 512, 256), (0, 768, 256)]
    + [(0, 512 * r, 512) for r in range(2, 8)]
    + [(1, 0, 512), (1, 512, 256), (1, 768, 128)]
)
NA = len(A_CHUNKS)
EVAC_LAG = 2
assert sum(C_SLOTS) == C_ITEMS + 2


def tile_haarwaveletlayer_t_kernel(tc, x, w_fusion, out):
    nc = tc.nc
    with ExitStack() as ctx:
        const = ctx.enter_context(tc.tile_pool(name="const", bufs=1))
        xpool = ctx.enter_context(tc.tile_pool(name="xpool", bufs=5))
        xcpool = ctx.enter_context(tc.tile_pool(name="xcpool", bufs=3))
        xrpool = ctx.enter_context(tc.tile_pool(name="xrpool", bufs=2))
        xtpool = ctx.enter_context(tc.tile_pool(name="xtpool", bufs=3))
        tpool = ctx.enter_context(tc.tile_pool(name="tpool", bufs=2))
        grpool = ctx.enter_context(tc.tile_pool(name="grpool", bufs=2))
        grcpool = ctx.enter_context(tc.tile_pool(name="grcpool", bufs=3))
        qpool = ctx.enter_context(tc.tile_pool(name="qpool", bufs=4))
        opool = ctx.enter_context(tc.tile_pool(name="opool", bufs=4))
        accpool = ctx.enter_context(tc.psum_pool(name="accpool", bufs=4))
        turnpool = ctx.enter_context(tc.psum_pool(name="turnpool", bufs=2))
        bandpool = ctx.enter_context(tc.psum_pool(name="bandpool", bufs=2))
        ctx.enter_context(tc.manual_schedule())

        x_tiles = {}
        xr_tiles = {}
        turn_tiles = {}
        turned_tiles = {}
        band_tiles = {}
        t_tiles = {}
        gr_tiles = {}
        q_tiles = {}
        out_tiles = {}
        filled = []

        def place(job):
            return (A_CHUNKS if job[0] == "a" else C_CHUNKS)[job[1]]

        def load(job):
            n, p0, npx = place(job)
            pixels = slice(4 * p0, 4 * (p0 + npx))
            if job[0] == "a":
                xt = xpool.tile([P, 2, 4 * npx], BF16, name="xt")
                src = x[n].rearrange("c h w -> c (h w)")[:, pixels]
                nc.sync.dma_start(out=xt[:, 0, :], in_=src[64:192])
                nc.sync.dma_start(out=xt[0:64, 1, :], in_=src[0:64])
                nc.sync.dma_start(out=xt[64:128, 1, :], in_=src[192:256])
            else:
                xt = xcpool.tile([P, 2, 4 * npx], BF16, name="xc")
                nc.sync.dma_start(out=xt[:], in_=x[n].rearrange("(g p) h w -> p g (h w)", g=2)[:, :, pixels])
            x_tiles[job] = xt

        def first_stage(i):
            npx = A_CHUNKS[i][2]
            xv = x_tiles[("a", i)][:].rearrange("p u (a d j e) -> p d u a j e", d=2, j=64, e=2)
            tt = tpool.tile([P, 2, 2, 2, npx], F32, name="tt")
            tv = tt[:].rearrange("p d u h (a j) -> p h d u a j", j=64)
            for h, op in ((0, ADD), (1, SUB)):
                nc.vector.tensor_tensor(
                    out=tv[:, h], in0=xv[:, :, :, :, :, 0], in1=xv[:, :, :, :, :, 1], op=op
                )
            t_tiles[i] = tt

        def second_stage(i):
            npx = A_CHUNKS[i][2]
            gr = grpool.tile([P, 2, 4 * npx], BF16, name="gr", align_bytes=64)
            tv = t_tiles[i][:].rearrange("p d u h (c i) -> p d c (u h) i", i=4)
            gv = gr[:].rearrange("p v (c i t) -> p v c t i", i=4, t=4)
            for v, op in ((0, ADD), (1, SUB)):
                nc.vector.tensor_tensor(out=gv[:, v], in0=tv[:, 0], in1=tv[:, 1], op=op)
            gr_tiles[("a", i)] = gr

        def split_rows(k):
            xr = xrpool.tile([P, 2, 2, C_CHUNKS[k][2] // 64, P], BF16, name="xr")
            src = x_tiles[("c", k)][:].bitcast(F32).rearrange("p g (r hh c) -> p hh (g r) c", hh=2, c=32)
            nc.scalar.copy(out=xr[:].bitcast(F32).rearrange("p hh g a (d c) -> p hh (g a d) c", d=2), in_=src)
            xr_tiles[k] = xr

        def turn(item):
            k, q = C_ITEM_LIST[item]
            if q == 0:
                split_rows(k)
            tb = turnpool.tile([P, 8, P], BF16, name="tb")
            for b in range(8):
                a, hh, g = 2 * q + b // 4, b // 2 % 2, b % 2
                nc.tensor.transpose(tb[:, b, :], xr_tiles[k][:, hh, g, a, :], identb[:])
            turn_tiles[item] = tb

        def take_turned(item):
            xt = xtpool.tile([P, 4, 256], BF16, name="turned")
            src = turn_tiles[item][:].rearrange("p b c -> p (b c)").bitcast(F32).rearrange("p (b q c) -> p b q c", q=4, c=32)
            dst = xt[:].bitcast(F32).rearrange("p b (q c) -> p b q c", c=32)
            nc.scalar.copy(out=dst[:, :, 0:2, :], in_=src[:, :, 0:4:3, :])
            nc.scalar.copy(out=dst[:, :, 2:4, :], in_=src[:, :, 1:3, :])
            turned_tiles[item] = xt

        def make_bands(item):
            bb = bandpool.tile([P, 2, 128, 2, 2], BF16, name="bb")
            for b in range(4):
                for u in range(2):
                    nc.tensor.matmul(
                        bb[:, :, 32 * b : 32 * (b + 1), u, :],
                        lhsT=turned_tiles[item][:, b, P * (1 - u) : P * (2 - u)],
                        rhs=haar[:],
                        start=True,
                        stop=True,
                    )
            band_tiles[item] = bb

        def take_bands(item):
            k, q = C_ITEM_LIST[item]
            if q == 0:
                gr_tiles[("c", k)] = grcpool.tile([P, 2, 4 * C_CHUNKS[k][2]], BF16, name="grc", align_bytes=64)
            nc.scalar.copy(
                out=gr_tiles[("c", k)][:, :, 512 * q : 512 * (q + 1)].bitcast(F32),
                in_=band_tiles[item][:].rearrange("p v x u h -> p v (x u h)").bitcast(F32),
            )

        def run_slot(slot):
            if slot < C_ITEMS:
                turn(slot)
            if 0 <= slot - 1 < C_ITEMS:
                take_turned(slot - 1)
                make_bands(slot - 1)
            if slot >= 2:
                take_bands(slot - 2)

        def quantise(job):
            npx = place(job)[2]
            codes = qpool.tile([P, 2 * npx], U32, name="codes", align_bytes=64)
            scales = qpool.tile([P, 2 * npx], U8, name="scales", align_bytes=64)
            nc.vector.quantize_mx(
                out=codes[:].bitcast(FP8X4), scales=scales[:], in_=gr_tiles[job][:].rearrange("p v f -> p (v f)")
            )
            q_tiles[job] = (codes, scales)

        def banks_of(job):
            npx = place(job)[2]
            return [(job, b) for b in range(MT * npx // BANK)]

        def multiply(job, b):
            npx = place(job)[2]
            codes, scales = q_tiles[job]
            per_bank = BANK // npx
            acc = accpool.tile([P, per_bank, npx], F32, name="acc", tag="acc")
            for s in range(per_bank):
                m = b * per_bank + s
                for s_k in range(2):
                    wcols = slice(512 * s_k + P * m, 512 * s_k + P * (m + 1))
                    xcols = slice(npx * s_k, npx * (s_k + 1))
                    nc.tensor.matmul_mx(
                        out=acc[:, s, :],
                        lhsT=w_codes[:, wcols].bitcast(FP8X4),
                        lhsT_scale=w_scales[:, wcols],
                        rhs=codes[:, xcols].bitcast(FP8X4),
                        rhs_scale=scales[:, xcols],
                        start=(s_k == 0),
                        stop=(s_k == 1),
                    )
            filled.append((job, b, acc))

        def evacuate(copy=nc.scalar.copy):
            job, b, acc = filled.pop(0)
            n, p0, npx = place(job)
            per_bank = BANK // npx
            if b == 0:
                out_tiles[job] = opool.tile([P, MT, npx], F32, name="ot", align_bytes=64)
            ot = out_tiles[job]
            copy(out=ot[:, b * per_bank : (b + 1) * per_bank, :], in_=acc[:])
            if b == MT // per_bank - 1:
                dst = out[n].rearrange("(m p) i j -> p m (i j)", m=MT)
                nc.scalar.dma_start(out=dst[:, :, p0 : p0 + npx], in_=ot[:])

        w_sb = const.tile([P, MT, 1024], BF16, name="w_sb")
        w_outer = const.tile([P, MT, 512], BF16, name="w_outer")
        w_codes = const.tile([P, 2 * 512], U32, name="w_codes", align_bytes=64)
        w_scales = const.tile([P, 2 * 512], U8, name="w_scales", align_bytes=64)

        def load_w():
            src = w_fusion.rearrange("(m p) k a b -> p m (k a b)", m=MT)
            nc.sync.dma_start(out=w_sb[:], in_=src)

        def copy_w_outer():
            quarters = w_sb[:].bitcast(F32).rearrange("p m (q k) -> p m q k", q=4)
            nc.scalar.copy(
                out=w_outer[:].bitcast(F32).rearrange("p m (q k) -> p m q k", q=2), in_=quarters[:, :, 0:4:3, :]
            )

        def transpose_w():
            wg = opool.tile([P, 2, 512 * 4], BF16, name="ot", align_bytes=64)
            for v in range(2):
                for oh in range(2):
                    wt = accpool.tile([P, 4, 256], BF16, name="wt", tag="acc")
                    for t in range(4):
                        u, h = divmod(t, 2)
                        first = 2 * h + v
                        for mm in range(2):
                            m = 2 * oh + mm
                            w_u = w_outer[:, m, :] if u else w_sb[:, m, 256:768]
                            nc.tensor.transpose(
                                wt[:, t, P * mm : P * (mm + 1)], w_u[:, first : first + 509 : 4], identb[:]
                            )
                    nc.scalar.activation(
                        out=wg[:, v, 1024 * oh : 1024 * (oh + 1)].rearrange("p (c i t) -> p c t i", i=4, t=4),
                        in_=wt[:].rearrange("p t (c i) -> p c t i", i=4),
                        func=COPY,
                        scale=0.5,
                    )
            return wg

        load(("a", 0))
        load(("a", 1))
        load(("a", 2))
        load(("c", 0))
        load_w()
        load(("a", 3))
        load(("c", 1))

        identb = const.tile([P, P], BF16, name="identb")
        make_identity(nc, identb[:])
        h2 = const.tile([P, 2, 32, 2], BF16, name="h2")
        haar = const.tile([P, 2, 32, 2], BF16, name="haar")
        iv = identb[:].rearrange("p (d j e) -> p d j e", d=2, e=2)
        for h, op in ((0, ADD), (1, SUB)):
            nc.vector.tensor_tensor(out=h2[:, :, :, h], in0=iv[:, :, :, 0], in1=iv[:, :, :, 1], op=op)
        for v, op in ((0, ADD), (1, SUB)):
            nc.vector.tensor_tensor(out=haar[:, v], in0=h2[:, 0], in1=h2[:, 1], op=op)

        first_stage(0)
        load(("a", 4))

        def evacuate_next(step):
            evacuate(nc.vector.tensor_copy if step >= NA and filled[0][1] % 2 else nc.scalar.copy)

        due = [[] for step in range(NA + 4)]
        slot = 0
        loaded_c = 2
        quantised_c = 0
        for i in range(NA + 3):
            done = C_ITEM_LIST[: max(slot - 2, 0)]
            started_c = C_ITEM_LIST[min(slot, C_ITEMS - 1)][0]
            if i + 1 < NA:
                first_stage(i + 1)
                if i + 5 < NA:
                    load(("a", i + 5))
            while loaded_c < len(C_CHUNKS) and loaded_c < started_c + 3:
                load(("c", loaded_c))
                loaded_c += 1
            if 1 <= i <= NA:
                quantise(("a", i - 1))
                due[max(i, 3)].append(("a", i - 1))
            if i < NA:
                second_stage(i)
            while quantised_c < len(C_CHUNKS) and (quantised_c, C_CHUNKS[quantised_c][2] // 128 - 1) in done:
                quantise(("c", quantised_c))
                due[max(i + 1, 3)].append(("c", quantised_c))
                quantised_c += 1
            if i == 1:
                copy_w_outer()
                w_grouped = transpose_w()
            if i == 2:
                nc.vector.quantize_mx(
                    out=w_codes[:].bitcast(FP8X4), scales=w_scales[:], in_=w_grouped[:].rearrange("p v f -> p (v f)")
                )
            banks = [bank for job in due[i] for bank in banks_of(job)]
            slots = C_SLOTS[i] if i < len(C_SLOTS) else 0
            for rep in range(slots + 1):
                for bank in banks[len(banks) * rep // (slots + 1) : len(banks) * (rep + 1) // (slots + 1)]:
                    multiply(*bank)
                    if len(filled) > EVAC_LAG:
                        evacuate_next(i)
                if rep < slots:
                    run_slot(slot)
                    slot += 1
        while filled:
            evacuate_next(NA + 3)
